import numpy as np
import ml_dtypes

BF16 = ml_dtypes.bfloat16


def bf(x):
    return np.asarray(x, np.float32).astype(BF16)


def f32(x):
    return np.asarray(x, np.float32)


def f64(x):
    return np.asarray(x).astype(np.float64)


def striped(idx):
    return np.tile(idx.reshape(-1, 16).T, (8, 1))


D, V, B, T, N = 1024, 2048, 4, 256, 1024
EPS = 1e-5


def sinusoidal(t, d):
    pos = np.arange(t, dtype=np.float32)[:, None]
    div = np.exp(np.arange(0, d, 2, dtype=np.float32) * np.float32(-np.log(10000.0) / d))
    pe = np.zeros((t, d), np.float32)
    pe[:, 0::2] = np.sin(pos * div)
    pe[:, 1::2] = np.cos(pos * div)
    return pe


def setup_inputs():
    r = np.random.standard_normal
    return {
        'tok_emb': f32(r((D, V))),
        'pos_enc': f32(np.tile(sinusoidal(T, D).T, (1, B))),
        'ln_gain': f32(1.0 + 0.1 * r((D, 1))),
        'ln_bias': f32(0.1 * r((D, 1))),
        'wq': bf(r((D, D)) / np.sqrt(D)),
        'bq': f32(0.1 * r((D, 1))),
        'wk': bf(r((D, D)) / np.sqrt(D)),
        'bk': f32(0.1 * r((D, 1))),
        'wv': bf(r((D, D)) / np.sqrt(D)),
        'bv': f32(0.1 * r((D, 1))),
        'offs': striped(np.random.permutation(np.tile(np.arange(V), 2))[:N]),
    }


def reference(tok_emb, pos_enc, ln_gain, ln_bias, wq, bq, wk, bk, wv, bv, offs):
    idx = offs[:16].T.reshape(-1)
    x = f64(tok_emb)[:, idx] + f64(pos_enc)
    mean = x.mean(axis=0, keepdims=True)
    var = np.square(x - mean).mean(axis=0, keepdims=True)
    h = (x - mean) / np.sqrt(var + EPS) * f64(ln_gain) + f64(ln_bias)
    q = f64(wq).T @ h + f64(bq)
    k = f64(wk).T @ h + f64(bk)
    v = f64(wv).T @ h + f64(bv)
    return np.concatenate([x, q, k, v], axis=0)

@@ -1,0 +1,137 @@
+from contextlib import ExitStack
+
+import concourse.mybir as mybir
+from concourse.masks import make_identity
+
+F32 = mybir.dt.float32
+BF16 = mybir.dt.bfloat16
+U16 = mybir.dt.uint16
+ALU = mybir.AluOpType
+ACT = mybir.ActivationFunctionType
+
+P = 128
+D = 1024
+V = 2048
+N = 1024
+KB = D // P
+CH = 512
+NCH = N // CH
+G = CH // P
+SIDE = 4
+STATS = 6
+EPS = 1e-5
+FLOPS = 3 * 2 * D * D * N
+
+
+def tile_decoderlm_b_kernel(
+    tc, tok_emb, pos_enc, ln_gain, ln_bias, wq, bq, wk, bk, wv, bv, offs, out
+):
+    nc = tc.nc
+    with ExitStack() as ctx:
+        held = ctx.enter_context(tc.tile_pool(name="held", bufs=1))
+        work = ctx.enter_context(tc.tile_pool(name="work", bufs=3))
+        stage = ctx.enter_context(tc.tile_pool(name="stage", bufs=6))
+        psum_flip = ctx.enter_context(tc.psum_pool(name="psum_flip", bufs=2))
+        psum_rows = ctx.enter_context(tc.psum_pool(name="psum_rows", bufs=1))
+        psum_acc = ctx.enter_context(tc.psum_pool(name="psum_acc", bufs=SIDE))
+
+        offsets = held.tile([P, N // 16], U16, name="offsets")
+        nc.sync.dma_start(offsets[:], offs)
+
+        tok = [held.tile([P, V], F32, name=f"tok{b}") for b in range(KB)]
+        pos = [[held.tile([P, CH], F32, name=f"pos{ch}_{b}") for b in range(KB)] for ch in range(NCH)]
+        weights = [held.tile([P, KB, D], BF16, name=f"w{pj}") for pj in range(3)]
+
+        for b in range(KB):
+            nc.sync.dma_start(tok[b][:], tok_emb[b * P : (b + 1) * P, :])
+            nc.sync.dma_start(pos[0][b][:], pos_enc[b * P : (b + 1) * P, 0:CH])
+        nc.sync.dma_start(weights[0][:], wq.rearrange("(kb p) m -> p kb m", p=P))
+        for b in range(KB):
+            nc.sync.dma_start(pos[1][b][:], pos_enc[b * P : (b + 1) * P, CH : 2 * CH])
+        nc.sync.dma_start(weights[1][:], wk.rearrange("(kb p) m -> p kb m", p=P))
+        nc.sync.dma_start(weights[2][:], wv.rearrange("(kb p) m -> p kb m", p=P))
+
+        ident = held.tile([P, P], F32, name="ident")
+        make_identity(nc, ident[:])
+        eps = held.tile([P, 1], F32, name="eps")
+        nc.vector.memset(eps[:], EPS)
+
+        vectors = (ln_gain, ln_bias, bq, bk, bv)
+        NV = len(vectors) * KB
+        vec_rows = held.tile([NV, P], F32, name="vec_rows")
+        for v, vec in enumerate(vectors):
+            nc.scalar.dma_start(
+                vec_rows[v * KB : (v + 1) * KB, :], vec.rearrange("(kb p) one -> kb (p one)", p=P)
+            )
+        vec_flip = psum_flip.tile([P, NV], F32, name="vec_flip", tag="flip")
+        nc.tensor.transpose(vec_flip[:], vec_rows[:], ident[0:NV, 0:NV])
+        vec_cols = held.tile([P, NV], F32, name="vec_cols")
+        nc.vector.tensor_copy(vec_cols[:], vec_flip[:])
+
+        x = [[held.tile([P, CH], F32, name=f"x{ch}_{b}") for b in range(KB)] for ch in range(NCH)]
+        h = [[held.tile([P, CH], BF16, name=f"h{ch}_{b}") for b in range(KB)] for ch in range(NCH)]
+
+        for ch in range(NCH):
+            piece = offsets[:, ch * (CH // 16) : (ch + 1) * (CH // 16)]
+            stats = held.tile([P, G, KB, STATS], F32, name=f"stats{ch}")
+            for b in range(KB):
+                nc.vector.tensor_tensor(x[ch][b][:], tok[b][:].indirect(piece), pos[ch][b][:], ALU.add)
+                nc.sync.dma_start(out[b * P : (b + 1) * P, ch * CH : (ch + 1) * CH], x[ch][b][:])
+                flip = psum_flip.tile([P, G, P], F32, name="flip", tag="flip")
+                for g in range(G):
+                    nc.tensor.transpose(flip[:, g, :], x[ch][b][:, g * P : (g + 1) * P], ident[:])
+                for g in range(G):
+                    nc.vector.bn_stats(stats[:, g, b, :], flip[:, g, :])
+
+            mean_var = held.tile([P, G, 2], F32, name=f"mean_var{ch}")
+            for g in range(G):
+                nc.vector.bn_aggr(mean_var[:, g, :], stats[:, g, :, :].rearrange("p b s -> p (b s)"))
+            std = held.tile([P, G, 1], F32, name=f"std{ch}")
+            nc.scalar.activation(std[:], mean_var[:, :, 1:2], ACT.Sqrt, bias=eps[:], scale=1.0)
+            rstd = held.tile([P, G, 1], F32, name=f"rstd{ch}")
+            nc.vector.reciprocal(rstd[:], std[:])
+
+            mean_row = psum_rows.tile([P, CH], F32, name="mean_row")
+            rstd_row = psum_rows.tile([P, CH], F32, name="rstd_row")
+            for g in range(G):
+                nc.tensor.transpose(
+                    mean_row[:, g * P : (g + 1) * P], mean_var[:, g, 0:1].to_broadcast([P, P]), ident[:]
+                )
+            for g in range(G):
+                nc.tensor.transpose(
+                    rstd_row[:, g * P : (g + 1) * P], rstd[:, g, :].to_broadcast([P, P]), ident[:]
+                )
+
+            for b in range(KB):
+                centred = work.tile([P, CH], F32, name="centred")
+                nc.vector.tensor_tensor(centred[:], x[ch][b][:], mean_row[:], ALU.subtract)
+                normed = work.tile([P, CH], F32, name="normed")
+                nc.vector.tensor_tensor(normed[:], centred[:], rstd_row[:], ALU.mult)
+                nc.scalar.activation(
+                    h[ch][b][:],
+                    normed[:],
+                    ACT.Identity,
+                    bias=vec_cols[:, KB + b : KB + b + 1],
+                    scale=vec_cols[:, b : b + 1],
+                )
+
+        blocks = [(pj, m) for pj in range(3) for m in range(KB)]
+        rounds = [(0, blocks[0:SIDE])] + [(0, [blk]) for blk in blocks[SIDE:]] + [(1, [blk]) for blk in blocks]
+
+        for ch, round_blocks in rounds:
+            acc = [psum_acc.tile([P, CH], F32, name=f"acc{pj}_{m}", tag="acc") for pj, m in round_blocks]
+            for kb in range(KB):
+                for a, (pj, m) in zip(acc, round_blocks):
+                    nc.tensor.matmul(
+                        a[:],
+                        weights[pj][:, kb, m * P : (m + 1) * P],
+                        h[ch][kb][:],
+                        start=(kb == 0),
+                        stop=(kb == KB - 1),
+                    )
+            for a, (pj, m) in zip(acc, round_blocks):
+                col = (2 + pj) * KB + m
+                res = stage.tile([P, CH], F32, name="res")
+                nc.scalar.activation(res[:], a[:], ACT.Identity, bias=vec_cols[:, col : col + 1], scale=1.0)
+                row = (1 + pj) * D + m * P
+                nc.sync.dma_start(out[row : row + P, ch * CH : (ch + 1) * CH], res[:])

@@ -14,10 +14,10 @@ D = 1024
 V = 2048
 N = 1024
 KB = D // P
-CH = 512
+CH = 256
 NCH = N // CH
 G = CH // P
-SIDE = 4
+ACC_BANKS = 5
 STATS = 6
 EPS = 1e-5
 FLOPS = 3 * 2 * D * D * N
@@ -33,23 +33,29 @@ def tile_decoderlm_b_kernel(
         stage = ctx.enter_context(tc.tile_pool(name="stage", bufs=6))
         psum_flip = ctx.enter_context(tc.psum_pool(name="psum_flip", bufs=2))
         psum_rows = ctx.enter_context(tc.psum_pool(name="psum_rows", bufs=1))
-        psum_acc = ctx.enter_context(tc.psum_pool(name="psum_acc", bufs=SIDE))
+        psum_acc = ctx.enter_context(tc.psum_pool(name="psum_acc", bufs=ACC_BANKS))
 
         offsets = held.tile([P, N // 16], U16, name="offsets")
         nc.sync.dma_start(offsets[:], offs)
 
         tok = [held.tile([P, V], F32, name=f"tok{b}") for b in range(KB)]
-        pos = [[held.tile([P, CH], F32, name=f"pos{ch}_{b}") for b in range(KB)] for ch in range(NCH)]
-        weights = [held.tile([P, KB, D], BF16, name=f"w{pj}") for pj in range(3)]
+        pos = [held.tile([P, KB, CH], F32, name=f"pos{ch}") for ch in range(NCH)]
+        weights = [[held.tile([P, D], BF16, name=f"w{pj}_{kb}") for kb in range(KB)] for pj in range(3)]
+        pos_chunks = [
+            pos_enc[:, ch * CH : (ch + 1) * CH].rearrange("(kb p) n -> p kb n", p=P) for ch in range(NCH)
+        ]
 
+        nc.sync.dma_start(pos[0][:], pos_chunks[0])
         for b in range(KB):
             nc.sync.dma_start(tok[b][:], tok_emb[b * P : (b + 1) * P, :])
-            nc.sync.dma_start(pos[0][b][:], pos_enc[b * P : (b + 1) * P, 0:CH])
-        nc.sync.dma_start(weights[0][:], wq.rearrange("(kb p) m -> p kb m", p=P))
-        for b in range(KB):
-            nc.sync.dma_start(pos[1][b][:], pos_enc[b * P : (b + 1) * P, CH : 2 * CH])
-        nc.sync.dma_start(weights[1][:], wk.rearrange("(kb p) m -> p kb m", p=P))
-        nc.sync.dma_start(weights[2][:], wv.rearrange("(kb p) m -> p kb m", p=P))
+        for kb in range(KB):
+            nc.sync.dma_start(weights[0][kb][:], wq[kb * P : (kb + 1) * P, :])
+        nc.sync.dma_start(pos[1][:], pos_chunks[1])
+        for pj, w in ((1, wk), (2, wv)):
+            for kb in range(KB):
+                nc.sync.dma_start(weights[pj][kb][:], w[kb * P : (kb + 1) * P, :])
+        nc.sync.dma_start(pos[2][:], pos_chunks[2])
+        nc.sync.dma_start(pos[3][:], pos_chunks[3])
 
         ident = held.tile([P, P], F32, name="ident")
         make_identity(nc, ident[:])
@@ -75,7 +81,7 @@ def tile_decoderlm_b_kernel(
             piece = offsets[:, ch * (CH // 16) : (ch + 1) * (CH // 16)]
             stats = held.tile([P, G, KB, STATS], F32, name=f"stats{ch}")
             for b in range(KB):
-                nc.vector.tensor_tensor(x[ch][b][:], tok[b][:].indirect(piece), pos[ch][b][:], ALU.add)
+                nc.vector.tensor_tensor(x[ch][b][:], tok[b][:].indirect(piece), pos[ch][:, b, :], ALU.add)
                 nc.sync.dma_start(out[b * P : (b + 1) * P, ch * CH : (ch + 1) * CH], x[ch][b][:])
                 flip = psum_flip.tile([P, G, P], F32, name="flip", tag="flip")
                 for g in range(G):
@@ -91,8 +97,9 @@ def tile_decoderlm_b_kernel(
             rstd = held.tile([P, G, 1], F32, name=f"rstd{ch}")
             nc.vector.reciprocal(rstd[:], std[:])
 
-            mean_row = psum_rows.tile([P, CH], F32, name="mean_row")
-            rstd_row = psum_rows.tile([P, CH], F32, name="rstd_row")
+            rows = psum_rows.tile([P, 2, CH], F32, name="rows")
+            mean_row = rows[:, 0, :]
+            rstd_row = rows[:, 1, :]
             for g in range(G):
                 nc.tensor.transpose(
                     mean_row[:, g * P : (g + 1) * P], mean_var[:, g, 0:1].to_broadcast([P, P]), ident[:]
@@ -104,9 +111,9 @@ def tile_decoderlm_b_kernel(
 
             for b in range(KB):
                 centred = work.tile([P, CH], F32, name="centred")
-                nc.vector.tensor_tensor(centred[:], x[ch][b][:], mean_row[:], ALU.subtract)
+                nc.vector.tensor_tensor(centred[:], x[ch][b][:], mean_row, ALU.subtract)
                 normed = work.tile([P, CH], F32, name="normed")
-                nc.vector.tensor_tensor(normed[:], centred[:], rstd_row[:], ALU.mult)
+                nc.vector.tensor_tensor(normed[:], centred[:], rstd_row, ALU.mult)
                 nc.scalar.activation(
                     h[ch][b][:],
                     normed[:],
@@ -116,7 +123,8 @@ def tile_decoderlm_b_kernel(
                 )
 
         blocks = [(pj, m) for pj in range(3) for m in range(KB)]
-        rounds = [(0, blocks[0:SIDE])] + [(0, [blk]) for blk in blocks[SIDE:]] + [(1, [blk]) for blk in blocks]
+        rounds = [(0, blocks[0:ACC_BANKS])] + [(0, [blk]) for blk in blocks[ACC_BANKS:]]
+        rounds += [(ch, [blk]) for ch in range(1, NCH) for blk in blocks]
 
         for ch, round_blocks in rounds:
             acc = [psum_acc.tile([P, CH], F32, name=f"acc{pj}_{m}", tag="acc") for pj, m in round_blocks]
@@ -124,7 +132,7 @@ def tile_decoderlm_b_kernel(
                 for a, (pj, m) in zip(acc, round_blocks):
                     nc.tensor.matmul(
                         a[:],
-                        weights[pj][:, kb, m * P : (m + 1) * P],
+                        weights[pj][kb][:, m * P : (m + 1) * P],
                         h[ch][kb][:],
                         start=(kb == 0),
                         stop=(kb == KB - 1),
@@ -134,4 +142,4 @@ def tile_decoderlm_b_kernel(
                 res = stage.tile([P, CH], F32, name="res")
                 nc.scalar.activation(res[:], a[:], ACT.Identity, bias=vec_cols[:, col : col + 1], scale=1.0)
                 row = (1 + pj) * D + m * P
-                nc.sync.dma_start(out[row : row + P, ch * CH : (ch + 1) * CH], res[:])
+                nc.scalar.dma_start(out[row : row + P, ch * CH : (ch + 1) * CH], res[:])

@@ -14,11 +14,11 @@ D = 1024
 V = 2048
 N = 1024
 KB = D // P
-CH = 256
-NCH = N // CH
-G = CH // P
-ACC_BANKS = 5
-STATS = 6
+BANK = 512
+CHUNKS = ((0, 128), (128, 128), (256, 256), (512, BANK))
+ROW_BANKS = 3
+ACC_BANKS = 8 - ROW_BANKS
+SIDE = 4
 EPS = 1e-5
 FLOPS = 3 * 2 * D * D * N
 
@@ -31,34 +31,35 @@ def tile_decoderlm_b_kernel(
         held = ctx.enter_context(tc.tile_pool(name="held", bufs=1))
         work = ctx.enter_context(tc.tile_pool(name="work", bufs=3))
         stage = ctx.enter_context(tc.tile_pool(name="stage", bufs=6))
-        psum_flip = ctx.enter_context(tc.psum_pool(name="psum_flip", bufs=2))
-        psum_rows = ctx.enter_context(tc.psum_pool(name="psum_rows", bufs=1))
+        psum_rows = ctx.enter_context(tc.psum_pool(name="psum_rows", bufs=ROW_BANKS))
         psum_acc = ctx.enter_context(tc.psum_pool(name="psum_acc", bufs=ACC_BANKS))
 
         offsets = held.tile([P, N // 16], U16, name="offsets")
         nc.sync.dma_start(offsets[:], offs)
 
         tok = [held.tile([P, V], F32, name=f"tok{b}") for b in range(KB)]
-        pos = [held.tile([P, KB, CH], F32, name=f"pos{ch}") for ch in range(NCH)]
-        weights = [[held.tile([P, D], BF16, name=f"w{pj}_{kb}") for kb in range(KB)] for pj in range(3)]
-        pos_chunks = [
-            pos_enc[:, ch * CH : (ch + 1) * CH].rearrange("(kb p) n -> p kb n", p=P) for ch in range(NCH)
+        pos = [
+            held.tile([P, KB, width], F32, name=f"pos{ch}", tag=f"pos_then_centred{ch}")
+            for ch, (first, width) in enumerate(CHUNKS)
         ]
+        weights = [held.tile([P, KB, D], BF16, name=f"w{pj}") for pj in range(3)]
+        by_block = "(kb p) n -> p kb n"
+        pos_dram = [pos_enc[:, first : first + width].rearrange(by_block, p=P) for first, width in CHUNKS]
 
-        nc.sync.dma_start(pos[0][:], pos_chunks[0])
+        nc.sync.dma_start(pos[0][:], pos_dram[0])
+        nc.sync.dma_start(pos[1][:], pos_dram[1])
         for b in range(KB):
             nc.sync.dma_start(tok[b][:], tok_emb[b * P : (b + 1) * P, :])
-        for kb in range(KB):
-            nc.sync.dma_start(weights[0][kb][:], wq[kb * P : (kb + 1) * P, :])
-        nc.sync.dma_start(pos[1][:], pos_chunks[1])
-        for pj, w in ((1, wk), (2, wv)):
-            for kb in range(KB):
-                nc.sync.dma_start(weights[pj][kb][:], w[kb * P : (kb + 1) * P, :])
-        nc.sync.dma_start(pos[2][:], pos_chunks[2])
-        nc.sync.dma_start(pos[3][:], pos_chunks[3])
+        nc.sync.dma_start(weights[0][:], wq.rearrange(by_block, p=P))
+        nc.sync.dma_start(pos[2][:], pos_dram[2])
+        nc.sync.dma_start(weights[1][:], wk.rearrange(by_block, p=P))
+        nc.sync.dma_start(weights[2][:], wv.rearrange(by_block, p=P))
+        nc.sync.dma_start(pos[3][:], pos_dram[3])
 
         ident = held.tile([P, P], F32, name="ident")
         make_identity(nc, ident[:])
+        averager = held.tile([P, P], F32, name="averager")
+        nc.vector.memset(averager[:], 1.0 / D)
         eps = held.tile([P, 1], F32, name="eps")
         nc.vector.memset(eps[:], EPS)
 
@@ -69,77 +70,79 @@ def tile_decoderlm_b_kernel(
             nc.scalar.dma_start(
                 vec_rows[v * KB : (v + 1) * KB, :], vec.rearrange("(kb p) one -> kb (p one)", p=P)
             )
-        vec_flip = psum_flip.tile([P, NV], F32, name="vec_flip", tag="flip")
+        vec_flip = psum_rows.tile([P, NV], F32, name="vec_flip", tag="row")
         nc.tensor.transpose(vec_flip[:], vec_rows[:], ident[0:NV, 0:NV])
         vec_cols = held.tile([P, NV], F32, name="vec_cols")
         nc.vector.tensor_copy(vec_cols[:], vec_flip[:])
 
-        x = [[held.tile([P, CH], F32, name=f"x{ch}_{b}") for b in range(KB)] for ch in range(NCH)]
-        h = [[held.tile([P, CH], BF16, name=f"h{ch}_{b}") for b in range(KB)] for ch in range(NCH)]
+        x = [held.tile([P, KB, width], F32, name=f"x{ch}") for ch, (first, width) in enumerate(CHUNKS)]
+        h = [held.tile([P, KB, width], BF16, name=f"h{ch}") for ch, (first, width) in enumerate(CHUNKS)]
 
-        for ch in range(NCH):
-            piece = offsets[:, ch * (CH // 16) : (ch + 1) * (CH // 16)]
-            stats = held.tile([P, G, KB, STATS], F32, name=f"stats{ch}")
+        for ch, (first, width) in enumerate(CHUNKS):
+            piece = offsets[:, first // 16 : (first + width) // 16]
+
+            x_sum = held.tile([P, width], F32, name=f"x_sum{ch}")
+            so_far = None
             for b in range(KB):
-                nc.vector.tensor_tensor(x[ch][b][:], tok[b][:].indirect(piece), pos[ch][:, b, :], ALU.add)
-                nc.sync.dma_start(out[b * P : (b + 1) * P, ch * CH : (ch + 1) * CH], x[ch][b][:])
-                flip = psum_flip.tile([P, G, P], F32, name="flip", tag="flip")
-                for g in range(G):
-                    nc.tensor.transpose(flip[:, g, :], x[ch][b][:, g * P : (g + 1) * P], ident[:])
-                for g in range(G):
-                    nc.vector.bn_stats(stats[:, g, b, :], flip[:, g, :])
+                nc.vector.tensor_tensor(x[ch][:, b, :], tok[b][:].indirect(piece), pos[ch][:, b, :], ALU.add)
+                if b == 0:
+                    so_far = x[ch][:, b, :]
+                else:
+                    nc.vector.tensor_tensor(x_sum[:], so_far, x[ch][:, b, :], ALU.add)
+                    so_far = x_sum[:]
+            nc.sync.dma_start(out[0:D, first : first + width].rearrange(by_block, p=P), x[ch][:])
+            mean_row = psum_rows.tile([P, width], F32, name="mean_row", tag="row")
+            nc.tensor.matmul(mean_row[:], averager[:], x_sum[:], start=True, stop=True)
 
-            mean_var = held.tile([P, G, 2], F32, name=f"mean_var{ch}")
-            for g in range(G):
-                nc.vector.bn_aggr(mean_var[:, g, :], stats[:, g, :, :].rearrange("p b s -> p (b s)"))
-            std = held.tile([P, G, 1], F32, name=f"std{ch}")
-            nc.scalar.activation(std[:], mean_var[:, :, 1:2], ACT.Sqrt, bias=eps[:], scale=1.0)
-            rstd = held.tile([P, G, 1], F32, name=f"rstd{ch}")
-            nc.vector.reciprocal(rstd[:], std[:])
+            centred = held.tile([P, KB, width], F32, name=f"centred{ch}", tag=f"pos_then_centred{ch}")
+            sq_sum = held.tile([P, width], F32, name=f"sq_sum{ch}")
+            so_far = None
+            for b in range(KB):
+                nc.vector.tensor_tensor(centred[:, b, :], x[ch][:, b, :], mean_row[:], ALU.subtract)
+                sq = work.tile([P, width], F32, name="sq")
+                nc.scalar.activation(sq[:], centred[:, b, :], ACT.Square)
+                if b == 0:
+                    so_far = sq[:]
+                else:
+                    nc.vector.tensor_tensor(sq_sum[:], so_far, sq[:], ALU.add)
+                    so_far = sq_sum[:]
+            var_row = psum_rows.tile([P, width], F32, name="var_row", tag="row")
+            nc.tensor.matmul(var_row[:], averager[:], sq_sum[:], start=True, stop=True)
 
-            rows = psum_rows.tile([P, 2, CH], F32, name="rows")
-            mean_row = rows[:, 0, :]
-            rstd_row = rows[:, 1, :]
-            for g in range(G):
-                nc.tensor.transpose(
-                    mean_row[:, g * P : (g + 1) * P], mean_var[:, g, 0:1].to_broadcast([P, P]), ident[:]
-                )
-            for g in range(G):
-                nc.tensor.transpose(
-                    rstd_row[:, g * P : (g + 1) * P], rstd[:, g, :].to_broadcast([P, P]), ident[:]
-                )
+            std_row = held.tile([P, width], F32, name=f"std_row{ch}")
+            nc.scalar.activation(std_row[:], var_row[:], ACT.Sqrt, bias=eps[:], scale=1.0)
+            rstd_row = held.tile([P, width], F32, name=f"rstd_row{ch}")
+            nc.vector.reciprocal(rstd_row[:], std_row[:])
 
             for b in range(KB):
-                centred = work.tile([P, CH], F32, name="centred")
-                nc.vector.tensor_tensor(centred[:], x[ch][b][:], mean_row, ALU.subtract)
-                normed = work.tile([P, CH], F32, name="normed")
-                nc.vector.tensor_tensor(normed[:], centred[:], rstd_row, ALU.mult)
+                nc.vector.tensor_tensor(centred[:, b, :], centred[:, b, :], rstd_row[:], ALU.mult)
                 nc.scalar.activation(
-                    h[ch][b][:],
-                    normed[:],
+                    h[ch][:, b, :],
+                    centred[:, b, :],
                     ACT.Identity,
                     bias=vec_cols[:, KB + b : KB + b + 1],
                     scale=vec_cols[:, b : b + 1],
                 )
 
         blocks = [(pj, m) for pj in range(3) for m in range(KB)]
-        rounds = [(0, blocks[0:ACC_BANKS])] + [(0, [blk]) for blk in blocks[ACC_BANKS:]]
-        rounds += [(ch, [blk]) for ch in range(1, NCH) for blk in blocks]
+        rounds = [(0, blocks[0:SIDE])] + [(0, [blk]) for blk in blocks[SIDE:]]
+        rounds += [(ch, [blk]) for ch in range(1, len(CHUNKS)) for blk in blocks]
 
         for ch, round_blocks in rounds:
-            acc = [psum_acc.tile([P, CH], F32, name=f"acc{pj}_{m}", tag="acc") for pj, m in round_blocks]
+            first, width = CHUNKS[ch]
+            acc = [psum_acc.tile([P, width], F32, name=f"acc{pj}_{m}", tag="acc") for pj, m in round_blocks]
             for kb in range(KB):
                 for a, (pj, m) in zip(acc, round_blocks):
                     nc.tensor.matmul(
                         a[:],
-                        weights[pj][kb][:, m * P : (m + 1) * P],
-                        h[ch][kb][:],
+                        weights[pj][:, kb, m * P : (m + 1) * P],
+                        h[ch][:, kb, :],
                         start=(kb == 0),
                         stop=(kb == KB - 1),
                     )
             for a, (pj, m) in zip(acc, round_blocks):
                 col = (2 + pj) * KB + m
-                res = stage.tile([P, CH], F32, name="res")
+                res = stage.tile([P, width], F32, name="res")
                 nc.scalar.activation(res[:], a[:], ACT.Identity, bias=vec_cols[:, col : col + 1], scale=1.0)
                 row = (1 + pj) * D + m * P
-                nc.scalar.dma_start(out[row : row + P, ch * CH : (ch + 1) * CH], res[:])
+                nc.scalar.dma_start(out[row : row + P, first : first + width], res[:])

@@ -14,13 +14,19 @@ D = 1024
 V = 2048
 N = 1024
 KB = D // P
-BANK = 512
-CHUNKS = ((0, 128), (128, 128), (256, 256), (512, BANK))
-ROW_BANKS = 3
-ACC_BANKS = 8 - ROW_BANKS
+CH = 256
+NCH = N // CH
+G = CH // P
+ACC_BANKS = 5
 SIDE = 4
+STATS = 6
 EPS = 1e-5
 FLOPS = 3 * 2 * D * D * N
+
+STEP_STATISTICS = KB
+STEP_ROWS = KB + 2
+STEP_NORMALISE = KB + 3
+STEPS = STEP_NORMALISE + KB
 
 
 def tile_decoderlm_b_kernel(
@@ -31,35 +37,31 @@ def tile_decoderlm_b_kernel(
         held = ctx.enter_context(tc.tile_pool(name="held", bufs=1))
         work = ctx.enter_context(tc.tile_pool(name="work", bufs=3))
         stage = ctx.enter_context(tc.tile_pool(name="stage", bufs=6))
-        psum_rows = ctx.enter_context(tc.psum_pool(name="psum_rows", bufs=ROW_BANKS))
+        psum_flip = ctx.enter_context(tc.psum_pool(name="psum_flip", bufs=2))
+        psum_rows = ctx.enter_context(tc.psum_pool(name="psum_rows", bufs=1))
         psum_acc = ctx.enter_context(tc.psum_pool(name="psum_acc", bufs=ACC_BANKS))
 
         offsets = held.tile([P, N // 16], U16, name="offsets")
         nc.sync.dma_start(offsets[:], offs)
 
         tok = [held.tile([P, V], F32, name=f"tok{b}") for b in range(KB)]
-        pos = [
-            held.tile([P, KB, width], F32, name=f"pos{ch}", tag=f"pos_then_centred{ch}")
-            for ch, (first, width) in enumerate(CHUNKS)
-        ]
+        pos = [held.tile([P, KB, CH], F32, name=f"pos{ch}") for ch in range(NCH)]
         weights = [held.tile([P, KB, D], BF16, name=f"w{pj}") for pj in range(3)]
         by_block = "(kb p) n -> p kb n"
-        pos_dram = [pos_enc[:, first : first + width].rearrange(by_block, p=P) for first, width in CHUNKS]
+        pos_dram = [pos_enc[:, ch * CH : (ch + 1) * CH].rearrange(by_block, p=P) for ch in range(NCH)]
 
         nc.sync.dma_start(pos[0][:], pos_dram[0])
-        nc.sync.dma_start(pos[1][:], pos_dram[1])
         for b in range(KB):
             nc.sync.dma_start(tok[b][:], tok_emb[b * P : (b + 1) * P, :])
         nc.sync.dma_start(weights[0][:], wq.rearrange(by_block, p=P))
-        nc.sync.dma_start(pos[2][:], pos_dram[2])
+        nc.sync.dma_start(pos[1][:], pos_dram[1])
         nc.sync.dma_start(weights[1][:], wk.rearrange(by_block, p=P))
         nc.sync.dma_start(weights[2][:], wv.rearrange(by_block, p=P))
+        nc.sync.dma_start(pos[2][:], pos_dram[2])
         nc.sync.dma_start(pos[3][:], pos_dram[3])
 
         ident = held.tile([P, P], F32, name="ident")
         make_identity(nc, ident[:])
-        averager = held.tile([P, P], F32, name="averager")
-        nc.vector.memset(averager[:], 1.0 / D)
         eps = held.tile([P, 1], F32, name="eps")
         nc.vector.memset(eps[:], EPS)
 
@@ -70,79 +72,89 @@ def tile_decoderlm_b_kernel(
             nc.scalar.dma_start(
                 vec_rows[v * KB : (v + 1) * KB, :], vec.rearrange("(kb p) one -> kb (p one)", p=P)
             )
-        vec_flip = psum_rows.tile([P, NV], F32, name="vec_flip", tag="row")
+        vec_flip = psum_flip.tile([P, NV], F32, name="vec_flip", tag="flip")
         nc.tensor.transpose(vec_flip[:], vec_rows[:], ident[0:NV, 0:NV])
         vec_cols = held.tile([P, NV], F32, name="vec_cols")
         nc.vector.tensor_copy(vec_cols[:], vec_flip[:])
 
-        x = [held.tile([P, KB, width], F32, name=f"x{ch}") for ch, (first, width) in enumerate(CHUNKS)]
-        h = [held.tile([P, KB, width], BF16, name=f"h{ch}") for ch, (first, width) in enumerate(CHUNKS)]
-
-        for ch, (first, width) in enumerate(CHUNKS):
-            piece = offsets[:, first // 16 : (first + width) // 16]
-
-            x_sum = held.tile([P, width], F32, name=f"x_sum{ch}")
-            so_far = None
-            for b in range(KB):
-                nc.vector.tensor_tensor(x[ch][:, b, :], tok[b][:].indirect(piece), pos[ch][:, b, :], ALU.add)
-                if b == 0:
-                    so_far = x[ch][:, b, :]
-                else:
-                    nc.vector.tensor_tensor(x_sum[:], so_far, x[ch][:, b, :], ALU.add)
-                    so_far = x_sum[:]
-            nc.sync.dma_start(out[0:D, first : first + width].rearrange(by_block, p=P), x[ch][:])
-            mean_row = psum_rows.tile([P, width], F32, name="mean_row", tag="row")
-            nc.tensor.matmul(mean_row[:], averager[:], x_sum[:], start=True, stop=True)
-
-            centred = held.tile([P, KB, width], F32, name=f"centred{ch}", tag=f"pos_then_centred{ch}")
-            sq_sum = held.tile([P, width], F32, name=f"sq_sum{ch}")
-            so_far = None
-            for b in range(KB):
-                nc.vector.tensor_tensor(centred[:, b, :], x[ch][:, b, :], mean_row[:], ALU.subtract)
-                sq = work.tile([P, width], F32, name="sq")
-                nc.scalar.activation(sq[:], centred[:, b, :], ACT.Square)
-                if b == 0:
-                    so_far = sq[:]
-                else:
-                    nc.vector.tensor_tensor(sq_sum[:], so_far, sq[:], ALU.add)
-                    so_far = sq_sum[:]
-            var_row = psum_rows.tile([P, width], F32, name="var_row", tag="row")
-            nc.tensor.matmul(var_row[:], averager[:], sq_sum[:], start=True, stop=True)
-
-            std_row = held.tile([P, width], F32, name=f"std_row{ch}")
-            nc.scalar.activation(std_row[:], var_row[:], ACT.Sqrt, bias=eps[:], scale=1.0)
-            rstd_row = held.tile([P, width], F32, name=f"rstd_row{ch}")
-            nc.vector.reciprocal(rstd_row[:], std_row[:])
-
-            for b in range(KB):
-                nc.vector.tensor_tensor(centred[:, b, :], centred[:, b, :], rstd_row[:], ALU.mult)
-                nc.scalar.activation(
-                    h[ch][:, b, :],
-                    centred[:, b, :],
-                    ACT.Identity,
-                    bias=vec_cols[:, KB + b : KB + b + 1],
-                    scale=vec_cols[:, b : b + 1],
-                )
+        x = [[held.tile([P, CH], F32, name=f"x{ch}_{b}") for b in range(KB)] for ch in range(NCH)]
+        h = [[held.tile([P, CH], BF16, name=f"h{ch}_{b}") for b in range(KB)] for ch in range(NCH)]
+        stats = [held.tile([P, G, KB, STATS], F32, name=f"stats{ch}") for ch in range(NCH)]
+        mean_var = [held.tile([P, G, 2], F32, name=f"mean_var{ch}") for ch in range(NCH)]
+        std = [held.tile([P, G, 1], F32, name=f"std{ch}") for ch in range(NCH)]
+        rstd = [held.tile([P, G, 1], F32, name=f"rstd{ch}") for ch in range(NCH)]
+        rows = None
 
         blocks = [(pj, m) for pj in range(3) for m in range(KB)]
-        rounds = [(0, blocks[0:SIDE])] + [(0, [blk]) for blk in blocks[SIDE:]]
-        rounds += [(ch, [blk]) for ch in range(1, len(CHUNKS)) for blk in blocks]
+        for ch in range(-1, NCH):
+            if ch < 0:
+                rounds = [[] for step in range(STEPS)]
+            elif ch == 0:
+                rounds = [blocks[0:SIDE]] + [[blk] for blk in blocks[SIDE:]]
+            else:
+                rounds = [[blk] for blk in blocks]
+            assert len(rounds) >= STEPS
 
-        for ch, round_blocks in rounds:
-            first, width = CHUNKS[ch]
-            acc = [psum_acc.tile([P, width], F32, name=f"acc{pj}_{m}", tag="acc") for pj, m in round_blocks]
-            for kb in range(KB):
+            for step, round_blocks in enumerate(rounds):
+                acc = [psum_acc.tile([P, CH], F32, name=f"acc{pj}_{m}", tag="acc") for pj, m in round_blocks]
+                for kb in range(KB):
+                    for a, (pj, m) in zip(acc, round_blocks):
+                        nc.tensor.matmul(
+                            a[:],
+                            weights[pj][:, kb, m * P : (m + 1) * P],
+                            h[ch][kb][:],
+                            start=(kb == 0),
+                            stop=(kb == KB - 1),
+                        )
                 for a, (pj, m) in zip(acc, round_blocks):
-                    nc.tensor.matmul(
-                        a[:],
-                        weights[pj][:, kb, m * P : (m + 1) * P],
-                        h[ch][:, kb, :],
-                        start=(kb == 0),
-                        stop=(kb == KB - 1),
+                    col = (2 + pj) * KB + m
+                    res = stage.tile([P, CH], F32, name="res")
+                    nc.scalar.activation(
+                        res[:], a[:], ACT.Identity, bias=vec_cols[:, col : col + 1], scale=1.0
                     )
-            for a, (pj, m) in zip(acc, round_blocks):
-                col = (2 + pj) * KB + m
-                res = stage.tile([P, width], F32, name="res")
-                nc.scalar.activation(res[:], a[:], ACT.Identity, bias=vec_cols[:, col : col + 1], scale=1.0)
-                row = (1 + pj) * D + m * P
-                nc.scalar.dma_start(out[row : row + P, first : first + width], res[:])
+                    row = (1 + pj) * D + m * P
+                    nc.scalar.dma_start(out[row : row + P, ch * CH : (ch + 1) * CH], res[:])
+
+                nx = ch + 1
+                if nx == NCH:
+                    continue
+                if step < STEP_STATISTICS:
+                    b = step
+                    piece = offsets[:, nx * (CH // 16) : (nx + 1) * (CH // 16)]
+                    nc.vector.tensor_tensor(x[nx][b][:], tok[b][:].indirect(piece), pos[nx][:, b, :], ALU.add)
+                    nc.sync.dma_start(out[b * P : (b + 1) * P, nx * CH : (nx + 1) * CH], x[nx][b][:])
+                    flip = psum_flip.tile([P, G, P], F32, name="flip", tag="flip")
+                    for g in range(G):
+                        nc.tensor.transpose(flip[:, g, :], x[nx][b][:, g * P : (g + 1) * P], ident[:])
+                    for g in range(G):
+                        nc.vector.bn_stats(stats[nx][:, g, b, :], flip[:, g, :])
+                elif step == STEP_STATISTICS:
+                    for g in range(G):
+                        nc.vector.bn_aggr(
+                            mean_var[nx][:, g, :], stats[nx][:, g, :, :].rearrange("p b s -> p (b s)")
+                        )
+                    nc.scalar.activation(std[nx][:], mean_var[nx][:, :, 1:2], ACT.Sqrt, bias=eps[:], scale=1.0)
+                    nc.vector.reciprocal(rstd[nx][:], std[nx][:])
+                elif step == STEP_ROWS:
+                    rows = psum_rows.tile([P, 2, CH], F32, name="rows")
+                    for g in range(G):
+                        nc.tensor.transpose(
+                            rows[:, 0, g * P : (g + 1) * P], mean_var[nx][:, g, 0:1].to_broadcast([P, P]), ident[:]
+                        )
+                    for g in range(G):
+                        nc.tensor.transpose(
+                            rows[:, 1, g * P : (g + 1) * P], rstd[nx][:, g, :].to_broadcast([P, P]), ident[:]
+                        )
+                elif STEP_NORMALISE <= step < STEPS:
+                    b = step - STEP_NORMALISE
+                    centred = work.tile([P, CH], F32, name="centred")
+                    nc.vector.tensor_tensor(centred[:], x[nx][b][:], rows[:, 0, :], ALU.subtract)
+                    normed = work.tile([P, CH], F32, name="normed")
+                    nc.vector.tensor_tensor(normed[:], centred[:], rows[:, 1, :], ALU.mult)
+                    nc.scalar.activation(
+                        h[nx][b][:],
+                        normed[:],
+                        ACT.Identity,
+                        bias=vec_cols[:, KB + b : KB + b + 1],
+                        scale=vec_cols[:, b : b + 1],
+                    )

@@ -17,16 +17,21 @@ KB = D // P
 CH = 256
 NCH = N // CH
 G = CH // P
-ACC_BANKS = 5
+PREP_BANKS = 3
+ACC_BANKS = 8 - PREP_BANKS
 SIDE = 4
+RING = 3
+STAGE = 20
 STATS = 6
 EPS = 1e-5
 FLOPS = 3 * 2 * D * D * N
 
-STEP_STATISTICS = KB
-STEP_ROWS = KB + 2
-STEP_NORMALISE = KB + 3
-STEPS = STEP_NORMALISE + KB
+PAIR = 2
+STEP_LOOK_UP = 0
+STEP_MEAN = 9
+STEP_CENTRE = 10
+STEP_VAR = 16
+STEP_SCALE = 17
 
 
 def tile_decoderlm_b_kernel(
@@ -36,9 +41,8 @@ def tile_decoderlm_b_kernel(
     with ExitStack() as ctx:
         held = ctx.enter_context(tc.tile_pool(name="held", bufs=1))
         work = ctx.enter_context(tc.tile_pool(name="work", bufs=3))
-        stage = ctx.enter_context(tc.tile_pool(name="stage", bufs=6))
-        psum_flip = ctx.enter_context(tc.psum_pool(name="psum_flip", bufs=2))
-        psum_rows = ctx.enter_context(tc.psum_pool(name="psum_rows", bufs=1))
+        stage = ctx.enter_context(tc.tile_pool(name="stage", bufs=STAGE))
+        psum_prep = ctx.enter_context(tc.psum_pool(name="psum_prep", bufs=PREP_BANKS))
         psum_acc = ctx.enter_context(tc.psum_pool(name="psum_acc", bufs=ACC_BANKS))
 
         offsets = held.tile([P, N // 16], U16, name="offsets")
@@ -62,6 +66,8 @@ def tile_decoderlm_b_kernel(
 
         ident = held.tile([P, P], F32, name="ident")
         make_identity(nc, ident[:])
+        averager = held.tile([P, P], F32, name="averager")
+        nc.vector.memset(averager[:], 1.0 / D)
         eps = held.tile([P, 1], F32, name="eps")
         nc.vector.memset(eps[:], EPS)
 
@@ -72,37 +78,69 @@ def tile_decoderlm_b_kernel(
             nc.scalar.dma_start(
                 vec_rows[v * KB : (v + 1) * KB, :], vec.rearrange("(kb p) one -> kb (p one)", p=P)
             )
-        vec_flip = psum_flip.tile([P, NV], F32, name="vec_flip", tag="flip")
+        vec_flip = psum_prep.tile([P, NV], F32, name="vec_flip", tag="prep")
         nc.tensor.transpose(vec_flip[:], vec_rows[:], ident[0:NV, 0:NV])
         vec_cols = held.tile([P, NV], F32, name="vec_cols")
         nc.vector.tensor_copy(vec_cols[:], vec_flip[:])
+        gain = [vec_cols[:, b : b + 1] for b in range(KB)]
+        bias = [vec_cols[:, KB + b : KB + b + 1] for b in range(KB)]
 
-        x = [[held.tile([P, CH], F32, name=f"x{ch}_{b}") for b in range(KB)] for ch in range(NCH)]
-        h = [[held.tile([P, CH], BF16, name=f"h{ch}_{b}") for b in range(KB)] for ch in range(NCH)]
-        stats = [held.tile([P, G, KB, STATS], F32, name=f"stats{ch}") for ch in range(NCH)]
-        mean_var = [held.tile([P, G, 2], F32, name=f"mean_var{ch}") for ch in range(NCH)]
-        std = [held.tile([P, G, 1], F32, name=f"std{ch}") for ch in range(NCH)]
-        rstd = [held.tile([P, G, 1], F32, name=f"rstd{ch}") for ch in range(NCH)]
-        rows = None
+        pieces = [offsets[:, ch * (CH // 16) : (ch + 1) * (CH // 16)] for ch in range(NCH)]
+        x_dram = [out[0:D, ch * CH : (ch + 1) * CH].rearrange(by_block, p=P) for ch in range(NCH)]
+
+        x = [None] * NCH
+        h = [None] * NCH
+        x[0] = held.tile([P, KB, CH], F32, name="x0", tag="ring0")
+        h[0] = held.tile([P, KB, CH], BF16, name="h0", tag="ring1")
+
+        stats = held.tile([P, G, KB, STATS], F32, name="stats")
+        for b in range(KB):
+            nc.vector.tensor_tensor(x[0][:, b, :], tok[b][:].indirect(pieces[0]), pos[0][:, b, :], ALU.add)
+            flip = psum_prep.tile([P, G, P], F32, name="flip", tag="prep")
+            for g in range(G):
+                nc.tensor.transpose(flip[:, g, :], x[0][:, b, g * P : (g + 1) * P], ident[:])
+            for g in range(G):
+                nc.vector.bn_stats(stats[:, g, b, :], flip[:, g, :])
+        nc.sync.dma_start(x_dram[0], x[0][:])
+
+        mean_var = held.tile([P, G, 2], F32, name="mean_var")
+        for g in range(G):
+            nc.vector.bn_aggr(mean_var[:, g, :], stats[:, g, :, :].rearrange("p b s -> p (b s)"))
+        std = held.tile([P, G, 1], F32, name="std")
+        nc.scalar.activation(std[:], mean_var[:, :, 1:2], ACT.Sqrt, bias=eps[:], scale=1.0)
+        rstd = held.tile([P, G, 1], F32, name="rstd")
+        nc.vector.reciprocal(rstd[:], std[:])
+
+        rows = psum_prep.tile([P, 2, CH], F32, name="rows", tag="prep")
+        for g in range(G):
+            nc.tensor.transpose(
+                rows[:, 0, g * P : (g + 1) * P], mean_var[:, g, 0:1].to_broadcast([P, P]), ident[:]
+            )
+        for g in range(G):
+            nc.tensor.transpose(rows[:, 1, g * P : (g + 1) * P], rstd[:, g, :].to_broadcast([P, P]), ident[:])
+
+        centred = held.tile([P, KB, CH], F32, name="centred0", tag="centred")
+        for b in range(KB):
+            nc.vector.tensor_tensor(centred[:, b, :], x[0][:, b, :], rows[:, 0, :], ALU.subtract)
+            nc.vector.tensor_tensor(centred[:, b, :], centred[:, b, :], rows[:, 1, :], ALU.mult)
+            nc.scalar.activation(h[0][:, b, :], centred[:, b, :], ACT.Identity, bias=bias[b], scale=gain[b])
 
         blocks = [(pj, m) for pj in range(3) for m in range(KB)]
-        for ch in range(-1, NCH):
-            if ch < 0:
-                rounds = [[] for step in range(STEPS)]
-            elif ch == 0:
-                rounds = [blocks[0:SIDE]] + [[blk] for blk in blocks[SIDE:]]
-            else:
-                rounds = [[blk] for blk in blocks]
-            assert len(rounds) >= STEPS
+        for ch in range(NCH):
+            side = SIDE if ch == 0 else 1
+            rounds = [blocks[0:side]] + [[blk] for blk in blocks[side:]]
+            nx = ch + 1
+            x_sum = sq_sum = mean_row = rstd_row = None
+            step = 0
 
-            for step, round_blocks in enumerate(rounds):
+            for round_blocks in rounds:
                 acc = [psum_acc.tile([P, CH], F32, name=f"acc{pj}_{m}", tag="acc") for pj, m in round_blocks]
                 for kb in range(KB):
                     for a, (pj, m) in zip(acc, round_blocks):
                         nc.tensor.matmul(
                             a[:],
                             weights[pj][:, kb, m * P : (m + 1) * P],
-                            h[ch][kb][:],
+                            h[ch][:, kb, :],
                             start=(kb == 0),
                             stop=(kb == KB - 1),
                         )
@@ -113,48 +151,48 @@ def tile_decoderlm_b_kernel(
                         res[:], a[:], ACT.Identity, bias=vec_cols[:, col : col + 1], scale=1.0
                     )
                     row = (1 + pj) * D + m * P
-                    nc.scalar.dma_start(out[row : row + P, ch * CH : (ch + 1) * CH], res[:])
+                    nc.sync.dma_start(out[row : row + P, ch * CH : (ch + 1) * CH], res[:])
 
-                nx = ch + 1
-                if nx == NCH:
-                    continue
-                if step < STEP_STATISTICS:
-                    b = step
-                    piece = offsets[:, nx * (CH // 16) : (nx + 1) * (CH // 16)]
-                    nc.vector.tensor_tensor(x[nx][b][:], tok[b][:].indirect(piece), pos[nx][:, b, :], ALU.add)
-                    nc.sync.dma_start(out[b * P : (b + 1) * P, nx * CH : (nx + 1) * CH], x[nx][b][:])
-                    flip = psum_flip.tile([P, G, P], F32, name="flip", tag="flip")
-                    for g in range(G):
-                        nc.tensor.transpose(flip[:, g, :], x[nx][b][:, g * P : (g + 1) * P], ident[:])
-                    for g in range(G):
-                        nc.vector.bn_stats(stats[nx][:, g, b, :], flip[:, g, :])
-                elif step == STEP_STATISTICS:
-                    for g in range(G):
-                        nc.vector.bn_aggr(
-                            mean_var[nx][:, g, :], stats[nx][:, g, :, :].rearrange("p b s -> p (b s)")
-                        )
-                    nc.scalar.activation(std[nx][:], mean_var[nx][:, :, 1:2], ACT.Sqrt, bias=eps[:], scale=1.0)
-                    nc.vector.reciprocal(rstd[nx][:], std[nx][:])
-                elif step == STEP_ROWS:
-                    rows = psum_rows.tile([P, 2, CH], F32, name="rows")
-                    for g in range(G):
-                        nc.tensor.transpose(
-                            rows[:, 0, g * P : (g + 1) * P], mean_var[nx][:, g, 0:1].to_broadcast([P, P]), ident[:]
-                        )
-                    for g in range(G):
-                        nc.tensor.transpose(
-                            rows[:, 1, g * P : (g + 1) * P], rstd[nx][:, g, :].to_broadcast([P, P]), ident[:]
-                        )
-                elif STEP_NORMALISE <= step < STEPS:
-                    b = step - STEP_NORMALISE
-                    centred = work.tile([P, CH], F32, name="centred")
-                    nc.vector.tensor_tensor(centred[:], x[nx][b][:], rows[:, 0, :], ALU.subtract)
-                    normed = work.tile([P, CH], F32, name="normed")
-                    nc.vector.tensor_tensor(normed[:], centred[:], rows[:, 1, :], ALU.mult)
-                    nc.scalar.activation(
-                        h[nx][b][:],
-                        normed[:],
-                        ACT.Identity,
-                        bias=vec_cols[:, KB + b : KB + b + 1],
-                        scale=vec_cols[:, b : b + 1],
-                    )
+                for blk in round_blocks:
+                    if nx == NCH:
+                        break
+                    if step == STEP_LOOK_UP:
+                        x[nx] = held.tile([P, KB, CH], F32, name=f"x{nx}", tag=f"ring{(2 * nx) % RING}")
+                        x_sum = held.tile([P, CH], F32, name=f"x_sum{nx}", tag="x_sum")
+                        for b in range(KB):
+                            nc.vector.tensor_tensor(
+                                x[nx][:, b, :], tok[b][:].indirect(pieces[nx]), pos[nx][:, b, :], ALU.add
+                            )
+                            if b > 0:
+                                so_far = x[nx][:, 0, :] if b == 1 else x_sum[:]
+                                nc.vector.tensor_tensor(x_sum[:], so_far, x[nx][:, b, :], ALU.add)
+                        nc.sync.dma_start(x_dram[nx], x[nx][:])
+                    elif step == STEP_MEAN:
+                        mean_row = psum_prep.tile([P, CH], F32, name="mean_row", tag="prep")
+                        nc.tensor.matmul(mean_row[:], averager[:], x_sum[:], start=True, stop=True)
+                        centred = held.tile([P, KB, CH], F32, name=f"centred{nx}", tag="centred")
+                        sq_sum = held.tile([P, CH], F32, name=f"sq_sum{nx}", tag="sq_sum")
+                    elif STEP_CENTRE <= step < STEP_CENTRE + KB // PAIR:
+                        for b in range((step - STEP_CENTRE) * PAIR, (step - STEP_CENTRE + 1) * PAIR):
+                            nc.vector.tensor_tensor(centred[:, b, :], x[nx][:, b, :], mean_row[:], ALU.subtract)
+                            if b == 0:
+                                nc.scalar.activation(sq_sum[:], centred[:, b, :], ACT.Square)
+                            else:
+                                sq = work.tile([P, CH], F32, name="sq")
+                                nc.scalar.activation(sq[:], centred[:, b, :], ACT.Square)
+                                nc.vector.tensor_tensor(sq_sum[:], sq_sum[:], sq[:], ALU.add)
+                    elif step == STEP_VAR:
+                        var_row = psum_prep.tile([P, CH], F32, name="var_row", tag="prep")
+                        nc.tensor.matmul(var_row[:], averager[:], sq_sum[:], start=True, stop=True)
+                        std_row = held.tile([P, CH], F32, name=f"std_row{nx}", tag="std_row")
+                        nc.scalar.activation(std_row[:], var_row[:], ACT.Sqrt, bias=eps[:], scale=1.0)
+                        rstd_row = held.tile([P, CH], F32, name=f"rstd_row{nx}", tag="rstd_row")
+                        nc.vector.reciprocal(rstd_row[:], std_row[:])
+                        h[nx] = held.tile([P, KB, CH], BF16, name=f"h{nx}", tag=f"ring{(2 * nx + 1) % RING}")
+                    elif STEP_SCALE <= step < STEP_SCALE + KB // PAIR:
+                        for b in range((step - STEP_SCALE) * PAIR, (step - STEP_SCALE + 1) * PAIR):
+                            nc.vector.tensor_tensor(centred[:, b, :], centred[:, b, :], rstd_row[:], ALU.mult)
+                            nc.scalar.activation(
+                                h[nx][:, b, :], centred[:, b, :], ACT.Identity, bias=bias[b], scale=gain[b]
+                            )
+                    step += 1

@@ -16,13 +16,11 @@ N = 1024
 KB = D // P
 CH = 256
 NCH = N // CH
-G = CH // P
 PREP_BANKS = 3
 ACC_BANKS = 8 - PREP_BANKS
 SIDE = 4
 RING = 3
 STAGE = 20
-STATS = 6
 EPS = 1e-5
 FLOPS = 3 * 2 * D * D * N
 
@@ -70,6 +68,8 @@ def tile_decoderlm_b_kernel(
         nc.vector.memset(averager[:], 1.0 / D)
         eps = held.tile([P, 1], F32, name="eps")
         nc.vector.memset(eps[:], EPS)
+        table_warm = held.tile([P, 1], F32, name="table_warm")
+        nc.scalar.activation(table_warm[:], eps[:], ACT.Abs_reciprocal_sqrt)
 
         vectors = (ln_gain, ln_bias, bq, bk, bv)
         NV = len(vectors) * KB
@@ -93,36 +93,27 @@ def tile_decoderlm_b_kernel(
         x[0] = held.tile([P, KB, CH], F32, name="x0", tag="ring0")
         h[0] = held.tile([P, KB, CH], BF16, name="h0", tag="ring1")
 
-        stats = held.tile([P, G, KB, STATS], F32, name="stats")
+        mean_row = psum_prep.tile([P, CH], F32, name="mean_row0", tag="prep")
+        sq_row = psum_prep.tile([P, CH], F32, name="sq_row0", tag="prep")
         for b in range(KB):
             nc.vector.tensor_tensor(x[0][:, b, :], tok[b][:].indirect(pieces[0]), pos[0][:, b, :], ALU.add)
-            flip = psum_prep.tile([P, G, P], F32, name="flip", tag="prep")
-            for g in range(G):
-                nc.tensor.transpose(flip[:, g, :], x[0][:, b, g * P : (g + 1) * P], ident[:])
-            for g in range(G):
-                nc.vector.bn_stats(stats[:, g, b, :], flip[:, g, :])
+            sq = work.tile([P, CH], F32, name="sq")
+            nc.scalar.activation(sq[:], x[0][:, b, :], ACT.Square)
+            nc.tensor.matmul(mean_row[:], averager[:], x[0][:, b, :], start=(b == 0), stop=(b == KB - 1))
+            nc.tensor.matmul(sq_row[:], averager[:], sq[:], start=(b == 0), stop=(b == KB - 1))
         nc.sync.dma_start(x_dram[0], x[0][:])
 
-        mean_var = held.tile([P, G, 2], F32, name="mean_var")
-        for g in range(G):
-            nc.vector.bn_aggr(mean_var[:, g, :], stats[:, g, :, :].rearrange("p b s -> p (b s)"))
-        std = held.tile([P, G, 1], F32, name="std")
-        nc.scalar.activation(std[:], mean_var[:, :, 1:2], ACT.Sqrt, bias=eps[:], scale=1.0)
-        rstd = held.tile([P, G, 1], F32, name="rstd")
-        nc.vector.reciprocal(rstd[:], std[:])
-
-        rows = psum_prep.tile([P, 2, CH], F32, name="rows", tag="prep")
-        for g in range(G):
-            nc.tensor.transpose(
-                rows[:, 0, g * P : (g + 1) * P], mean_var[:, g, 0:1].to_broadcast([P, P]), ident[:]
-            )
-        for g in range(G):
-            nc.tensor.transpose(rows[:, 1, g * P : (g + 1) * P], rstd[:, g, :].to_broadcast([P, P]), ident[:])
+        mean_sq = held.tile([P, CH], F32, name="mean_sq0", tag="mean_sq")
+        nc.scalar.activation(mean_sq[:], mean_row[:], ACT.Square)
+        var = held.tile([P, CH], F32, name="var0", tag="std_row")
+        nc.vector.tensor_tensor(var[:], sq_row[:], mean_sq[:], ALU.subtract)
+        rstd_row = held.tile([P, CH], F32, name="rstd_row0", tag="rstd_row")
+        nc.scalar.activation(rstd_row[:], var[:], ACT.Abs_reciprocal_sqrt, bias=eps[:], scale=1.0)
 
         centred = held.tile([P, KB, CH], F32, name="centred0", tag="centred")
         for b in range(KB):
-            nc.vector.tensor_tensor(centred[:, b, :], x[0][:, b, :], rows[:, 0, :], ALU.subtract)
-            nc.vector.tensor_tensor(centred[:, b, :], centred[:, b, :], rows[:, 1, :], ALU.mult)
+            nc.vector.tensor_tensor(centred[:, b, :], x[0][:, b, :], mean_row[:], ALU.subtract)
+            nc.vector.tensor_tensor(centred[:, b, :], centred[:, b, :], rstd_row[:], ALU.mult)
             nc.scalar.activation(h[0][:, b, :], centred[:, b, :], ACT.Identity, bias=bias[b], scale=gain[b])
 
         blocks = [(pj, m) for pj in range(3) for m in range(KB)]
@@ -184,10 +175,8 @@ def tile_decoderlm_b_kernel(
                     elif step == STEP_VAR:
                         var_row = psum_prep.tile([P, CH], F32, name="var_row", tag="prep")
                         nc.tensor.matmul(var_row[:], averager[:], sq_sum[:], start=True, stop=True)
-                        std_row = held.tile([P, CH], F32, name=f"std_row{nx}", tag="std_row")
-                        nc.scalar.activation(std_row[:], var_row[:], ACT.Sqrt, bias=eps[:], scale=1.0)
                         rstd_row = held.tile([P, CH], F32, name=f"rstd_row{nx}", tag="rstd_row")
-                        nc.vector.reciprocal(rstd_row[:], std_row[:])
+                        nc.scalar.activation(rstd_row[:], var_row[:], ACT.Abs_reciprocal_sqrt, bias=eps[:], scale=1.0)
                         h[nx] = held.tile([P, KB, CH], BF16, name=f"h{nx}", tag=f"ring{(2 * nx + 1) % RING}")
                     elif STEP_SCALE <= step < STEP_SCALE + KB // PAIR:
                         for b in range((step - STEP_SCALE) * PAIR, (step - STEP_SCALE + 1) * PAIR):

@@ -8,6 +8,7 @@ BF16 = mybir.dt.bfloat16
 U16 = mybir.dt.uint16
 ALU = mybir.AluOpType
 ACT = mybir.ActivationFunctionType
+AX = mybir.AxisListType
 
 P = 128
 D = 1024
@@ -16,6 +17,7 @@ N = 1024
 KB = D // P
 CH = 256
 NCH = N // CH
+SQ = 32
 PREP_BANKS = 3
 ACC_BANKS = 8 - PREP_BANKS
 SIDE = 4
@@ -26,10 +28,10 @@ FLOPS = 3 * 2 * D * D * N
 
 PAIR = 2
 STEP_LOOK_UP = 0
-STEP_MEAN = 9
-STEP_CENTRE = 10
-STEP_VAR = 16
-STEP_SCALE = 17
+STEP_MEAN = 10
+STEP_CENTRE = 11
+STEP_VAR = 18
+STEP_SCALE = 19
 
 
 def tile_decoderlm_b_kernel(
@@ -66,6 +68,14 @@ def tile_decoderlm_b_kernel(
         make_identity(nc, ident[:])
         averager = held.tile([P, P], F32, name="averager")
         nc.vector.memset(averager[:], 1.0 / D)
+        strip = held.tile([P, SQ], F32, name="strip")
+        nc.vector.tensor_reduce(strip[:], ident[:].rearrange("p (c j) -> p j c", j=SQ), AX.X, ALU.add)
+        fold = held.tile([P, P], F32, name="fold")
+        nc.vector.tensor_scalar_mul(
+            fold[:].rearrange("p (c j) -> p c j", j=SQ),
+            strip[:].unsqueeze(1).to_broadcast([P, P // SQ, SQ]),
+            1.0 / D,
+        )
         eps = held.tile([P, 1], F32, name="eps")
         nc.vector.memset(eps[:], EPS)
         table_warm = held.tile([P, 1], F32, name="table_warm")
@@ -84,6 +94,28 @@ def tile_decoderlm_b_kernel(
         nc.vector.tensor_copy(vec_cols[:], vec_flip[:])
         gain = [vec_cols[:, b : b + 1] for b in range(KB)]
         bias = [vec_cols[:, KB + b : KB + b + 1] for b in range(KB)]
+
+        def pack(total, what):
+            flipped = held.tile([P, CH], F32, name=f"flipped_{what}", tag="flipped", align_bytes=64)
+            nc.vector.transpose(flipped[:], total[:])
+            packed = held.tile([P, CH // SQ], F32, name=f"packed_{what}", tag="packed")
+            nc.vector.tensor_reduce(packed[:], flipped[:].rearrange("p (c j) -> p c j", j=SQ), AX.X, ALU.add)
+            return packed
+
+        def spread(packed, func, func_bias, what):
+            means = psum_prep.tile([P, CH // SQ], F32, name=f"means_{what}", tag="prep")
+            nc.tensor.matmul(means[:], fold[:], packed[:], start=True, stop=True)
+            repeated = held.tile([P, CH], F32, name=f"repeated_{what}", tag="repeated", align_bytes=64)
+            nc.scalar.activation(
+                repeated[:].rearrange("p (c j) -> p c j", j=SQ),
+                means[:].unsqueeze(2).to_broadcast([P, CH // SQ, SQ]),
+                func,
+                bias=func_bias,
+                scale=1.0,
+            )
+            row = held.tile([P, CH], F32, name=f"row_{what}", tag=f"row_{what}", align_bytes=64)
+            nc.vector.transpose(row[:], repeated[:])
+            return row
 
         pieces = [offsets[:, ch * (CH // 16) : (ch + 1) * (CH // 16)] for ch in range(NCH)]
         x_dram = [out[0:D, ch * CH : (ch + 1) * CH].rearrange(by_block, p=P) for ch in range(NCH)]
@@ -118,10 +150,9 @@ def tile_decoderlm_b_kernel(
 
         blocks = [(pj, m) for pj in range(3) for m in range(KB)]
         for ch in range(NCH):
-            side = SIDE if ch == 0 else 1
-            rounds = [blocks[0:side]] + [[blk] for blk in blocks[side:]]
+            rounds = [blocks[0:SIDE]] + [[blk] for blk in blocks[SIDE:]]
             nx = ch + 1
-            x_sum = sq_sum = mean_row = rstd_row = None
+            x_sum = sq_sum = packed = mean_row = rstd_row = None
             step = 0
 
             for round_blocks in rounds:
@@ -149,7 +180,7 @@ def tile_decoderlm_b_kernel(
                         break
                     if step == STEP_LOOK_UP:
                         x[nx] = held.tile([P, KB, CH], F32, name=f"x{nx}", tag=f"ring{(2 * nx) % RING}")
-                        x_sum = held.tile([P, CH], F32, name=f"x_sum{nx}", tag="x_sum")
+                        x_sum = held.tile([P, CH], F32, name=f"x_sum{nx}", tag="x_sum", align_bytes=64)
                         for b in range(KB):
                             nc.vector.tensor_tensor(
                                 x[nx][:, b, :], tok[b][:].indirect(pieces[nx]), pos[nx][:, b, :], ALU.add
@@ -158,11 +189,11 @@ def tile_decoderlm_b_kernel(
                                 so_far = x[nx][:, 0, :] if b == 1 else x_sum[:]
                                 nc.vector.tensor_tensor(x_sum[:], so_far, x[nx][:, b, :], ALU.add)
                         nc.sync.dma_start(x_dram[nx], x[nx][:])
+                        packed = pack(x_sum, "mean")
                     elif step == STEP_MEAN:
-                        mean_row = psum_prep.tile([P, CH], F32, name="mean_row", tag="prep")
-                        nc.tensor.matmul(mean_row[:], averager[:], x_sum[:], start=True, stop=True)
+                        mean_row = spread(packed, ACT.Identity, 0.0, "mean")
                         centred = held.tile([P, KB, CH], F32, name=f"centred{nx}", tag="centred")
-                        sq_sum = held.tile([P, CH], F32, name=f"sq_sum{nx}", tag="sq_sum")
+                        sq_sum = held.tile([P, CH], F32, name=f"sq_sum{nx}", tag="sq_sum", align_bytes=64)
                     elif STEP_CENTRE <= step < STEP_CENTRE + KB // PAIR:
                         for b in range((step - STEP_CENTRE) * PAIR, (step - STEP_CENTRE + 1) * PAIR):
                             nc.vector.tensor_tensor(centred[:, b, :], x[nx][:, b, :], mean_row[:], ALU.subtract)
@@ -172,11 +203,10 @@ def tile_decoderlm_b_kernel(
                                 sq = work.tile([P, CH], F32, name="sq")
                                 nc.scalar.activation(sq[:], centred[:, b, :], ACT.Square)
                                 nc.vector.tensor_tensor(sq_sum[:], sq_sum[:], sq[:], ALU.add)
+                        if step == STEP_CENTRE + KB // PAIR - 1:
+                            packed = pack(sq_sum, "var")
                     elif step == STEP_VAR:
-                        var_row = psum_prep.tile([P, CH], F32, name="var_row", tag="prep")
-                        nc.tensor.matmul(var_row[:], averager[:], sq_sum[:], start=True, stop=True)
-                        rstd_row = held.tile([P, CH], F32, name=f"rstd_row{nx}", tag="rstd_row")
-                        nc.scalar.activation(rstd_row[:], var_row[:], ACT.Abs_reciprocal_sqrt, bias=eps[:], scale=1.0)
+                        rstd_row = spread(packed, ACT.Abs_reciprocal_sqrt, eps[:], "rstd")
                         h[nx] = held.tile([P, KB, CH], BF16, name=f"h{nx}", tag=f"ring{(2 * nx + 1) % RING}")
                     elif STEP_SCALE <= step < STEP_SCALE + KB // PAIR:
                         for b in range((step - STEP_SCALE) * PAIR, (step - STEP_SCALE + 1) * PAIR):

@@ -68,6 +68,8 @@ def tile_decoderlm_b_kernel(
         make_identity(nc, ident[:])
         averager = held.tile([P, P], F32, name="averager")
         nc.vector.memset(averager[:], 1.0 / D)
+        block_averager = held.tile([P, P], F32, name="block_averager")
+        nc.vector.memset(block_averager[:], 1.0 / P)
         strip = held.tile([P, SQ], F32, name="strip")
         nc.vector.tensor_reduce(strip[:], ident[:].rearrange("p (c j) -> p j c", j=SQ), AX.X, ALU.add)
         fold = held.tile([P, P], F32, name="fold")
@@ -125,13 +127,18 @@ def tile_decoderlm_b_kernel(
         x[0] = held.tile([P, KB, CH], F32, name="x0", tag="ring0")
         h[0] = held.tile([P, KB, CH], BF16, name="h0", tag="ring1")
 
+        shift_row = psum_prep.tile([P, CH], F32, name="shift_row0", tag="prep")
         mean_row = psum_prep.tile([P, CH], F32, name="mean_row0", tag="prep")
         sq_row = psum_prep.tile([P, CH], F32, name="sq_row0", tag="prep")
+        centred = held.tile([P, KB, CH], F32, name="centred0", tag="centred")
         for b in range(KB):
             nc.vector.tensor_tensor(x[0][:, b, :], tok[b][:].indirect(pieces[0]), pos[0][:, b, :], ALU.add)
+            if b == 0:
+                nc.tensor.matmul(shift_row[:], block_averager[:], x[0][:, 0, :], start=True, stop=True)
+            nc.vector.tensor_tensor(centred[:, b, :], x[0][:, b, :], shift_row[:], ALU.subtract)
             sq = work.tile([P, CH], F32, name="sq")
-            nc.scalar.activation(sq[:], x[0][:, b, :], ACT.Square)
-            nc.tensor.matmul(mean_row[:], averager[:], x[0][:, b, :], start=(b == 0), stop=(b == KB - 1))
+            nc.vector.tensor_tensor(sq[:], centred[:, b, :], centred[:, b, :], ALU.mult)
+            nc.tensor.matmul(mean_row[:], averager[:], centred[:, b, :], start=(b == 0), stop=(b == KB - 1))
             nc.tensor.matmul(sq_row[:], averager[:], sq[:], start=(b == 0), stop=(b == KB - 1))
         nc.sync.dma_start(x_dram[0], x[0][:])
 
@@ -142,11 +149,13 @@ def tile_decoderlm_b_kernel(
         rstd_row = held.tile([P, CH], F32, name="rstd_row0", tag="rstd_row")
         nc.scalar.activation(rstd_row[:], var[:], ACT.Abs_reciprocal_sqrt, bias=eps[:], scale=1.0)
 
-        centred = held.tile([P, KB, CH], F32, name="centred0", tag="centred")
         for b in range(KB):
-            nc.vector.tensor_tensor(centred[:, b, :], x[0][:, b, :], mean_row[:], ALU.subtract)
+            nc.vector.tensor_tensor(centred[:, b, :], centred[:, b, :], mean_row[:], ALU.subtract)
             nc.vector.tensor_tensor(centred[:, b, :], centred[:, b, :], rstd_row[:], ALU.mult)
-            nc.scalar.activation(h[0][:, b, :], centred[:, b, :], ACT.Identity, bias=bias[b], scale=gain[b])
+            if b == 0:
+                nc.vector.tensor_scalar(h[0][:, b, :], centred[:, b, :], gain[b], bias[b], ALU.mult, ALU.add)
+            else:
+                nc.scalar.activation(h[0][:, b, :], centred[:, b, :], ACT.Identity, bias=bias[b], scale=gain[b])
 
         blocks = [(pj, m) for pj in range(3) for m in range(KB)]
         for ch in range(NCH):

@@ -131,15 +131,24 @@ def tile_decoderlm_b_kernel(
         mean_row = psum_prep.tile([P, CH], F32, name="mean_row0", tag="prep")
         sq_row = psum_prep.tile([P, CH], F32, name="sq_row0", tag="prep")
         centred = held.tile([P, KB, CH], F32, name="centred0", tag="centred")
+        pos_shifted = held.tile([P, KB, CH], F32, name="pos_shifted")
         for b in range(KB):
-            nc.vector.tensor_tensor(x[0][:, b, :], tok[b][:].indirect(pieces[0]), pos[0][:, b, :], ALU.add)
             if b == 0:
+                nc.vector.tensor_tensor(x[0][:, b, :], tok[b][:].indirect(pieces[0]), pos[0][:, b, :], ALU.add)
                 nc.tensor.matmul(shift_row[:], block_averager[:], x[0][:, 0, :], start=True, stop=True)
-            nc.vector.tensor_tensor(centred[:, b, :], x[0][:, b, :], shift_row[:], ALU.subtract)
+                nc.vector.tensor_tensor(centred[:, b, :], x[0][:, b, :], shift_row[:], ALU.subtract)
+                for later in range(1, KB):
+                    nc.vector.tensor_tensor(pos_shifted[:, later, :], pos[0][:, later, :], shift_row[:], ALU.subtract)
+            else:
+                nc.vector.tensor_tensor(
+                    centred[:, b, :], tok[b][:].indirect(pieces[0]), pos_shifted[:, b, :], ALU.add
+                )
             sq = work.tile([P, CH], F32, name="sq")
             nc.vector.tensor_tensor(sq[:], centred[:, b, :], centred[:, b, :], ALU.mult)
             nc.tensor.matmul(mean_row[:], averager[:], centred[:, b, :], start=(b == 0), stop=(b == KB - 1))
             nc.tensor.matmul(sq_row[:], averager[:], sq[:], start=(b == 0), stop=(b == KB - 1))
+            if b > 0:
+                nc.vector.tensor_tensor(x[0][:, b, :], tok[b][:].indirect(pieces[0]), pos[0][:, b, :], ALU.add)
         nc.sync.dma_start(x_dram[0], x[0][:])
 
         mean_sq = held.tile([P, CH], F32, name="mean_sq0", tag="mean_sq")

@@ -68,8 +68,8 @@ def tile_decoderlm_b_kernel(
         make_identity(nc, ident[:])
         averager = held.tile([P, P], F32, name="averager")
         nc.vector.memset(averager[:], 1.0 / D)
-        block_averager = held.tile([P, P], F32, name="block_averager")
-        nc.vector.memset(block_averager[:], 1.0 / P)
+        minus_block_averager = held.tile([P, P], F32, name="minus_block_averager")
+        nc.vector.memset(minus_block_averager[:], -1.0 / P)
         strip = held.tile([P, SQ], F32, name="strip")
         nc.vector.tensor_reduce(strip[:], ident[:].rearrange("p (c j) -> p j c", j=SQ), AX.X, ALU.add)
         fold = held.tile([P, P], F32, name="fold")
@@ -135,10 +135,10 @@ def tile_decoderlm_b_kernel(
         for b in range(KB):
             if b == 0:
                 nc.vector.tensor_tensor(x[0][:, b, :], tok[b][:].indirect(pieces[0]), pos[0][:, b, :], ALU.add)
-                nc.tensor.matmul(shift_row[:], block_averager[:], x[0][:, 0, :], start=True, stop=True)
-                nc.vector.tensor_tensor(centred[:, b, :], x[0][:, b, :], shift_row[:], ALU.subtract)
+                nc.tensor.matmul(shift_row[:], minus_block_averager[:], x[0][:, 0, :], start=True, stop=True)
+                nc.vector.tensor_tensor(centred[:, b, :], x[0][:, b, :], shift_row[:], ALU.add)
                 for later in range(1, KB):
-                    nc.vector.tensor_tensor(pos_shifted[:, later, :], pos[0][:, later, :], shift_row[:], ALU.subtract)
+                    nc.vector.tensor_tensor(pos_shifted[:, later, :], pos[0][:, later, :], shift_row[:], ALU.add)
             else:
                 nc.vector.tensor_tensor(
                     centred[:, b, :], tok[b][:].indirect(pieces[0]), pos_shifted[:, b, :], ALU.add
@@ -146,17 +146,16 @@ def tile_decoderlm_b_kernel(
             sq = work.tile([P, CH], F32, name="sq")
             nc.vector.tensor_tensor(sq[:], centred[:, b, :], centred[:, b, :], ALU.mult)
             nc.tensor.matmul(mean_row[:], averager[:], centred[:, b, :], start=(b == 0), stop=(b == KB - 1))
-            nc.tensor.matmul(sq_row[:], averager[:], sq[:], start=(b == 0), stop=(b == KB - 1))
+            nc.tensor.matmul(sq_row[:], averager[:], sq[:], start=(b == 0), stop=False)
             if b > 0:
                 nc.vector.tensor_tensor(x[0][:, b, :], tok[b][:].indirect(pieces[0]), pos[0][:, b, :], ALU.add)
         nc.sync.dma_start(x_dram[0], x[0][:])
 
         mean_sq = held.tile([P, CH], F32, name="mean_sq0", tag="mean_sq")
         nc.scalar.activation(mean_sq[:], mean_row[:], ACT.Square)
-        var = held.tile([P, CH], F32, name="var0", tag="std_row")
-        nc.vector.tensor_tensor(var[:], sq_row[:], mean_sq[:], ALU.subtract)
+        nc.tensor.matmul(sq_row[:], minus_block_averager[:], mean_sq[:], start=False, stop=True)
         rstd_row = held.tile([P, CH], F32, name="rstd_row0", tag="rstd_row")
-        nc.scalar.activation(rstd_row[:], var[:], ACT.Abs_reciprocal_sqrt, bias=eps[:], scale=1.0)
+        nc.scalar.activation(rstd_row[:], sq_row[:], ACT.Abs_reciprocal_sqrt, bias=eps[:], scale=1.0)
 
         for b in range(KB):
             nc.vector.tensor_tensor(centred[:, b, :], centred[:, b, :], mean_row[:], ALU.subtract)

@@ -155,15 +155,20 @@ def tile_decoderlm_b_kernel(
         nc.scalar.activation(mean_sq[:], mean_row[:], ACT.Square)
         nc.tensor.matmul(sq_row[:], minus_block_averager[:], mean_sq[:], start=False, stop=True)
         rstd_row = held.tile([P, CH], F32, name="rstd_row0", tag="rstd_row")
-        nc.scalar.activation(rstd_row[:], sq_row[:], ACT.Abs_reciprocal_sqrt, bias=eps[:], scale=1.0)
-
-        for b in range(KB):
-            nc.vector.tensor_tensor(centred[:, b, :], centred[:, b, :], mean_row[:], ALU.subtract)
-            nc.vector.tensor_tensor(centred[:, b, :], centred[:, b, :], rstd_row[:], ALU.mult)
-            if b == 0:
-                nc.vector.tensor_scalar(h[0][:, b, :], centred[:, b, :], gain[b], bias[b], ALU.mult, ALU.add)
-            else:
-                nc.scalar.activation(h[0][:, b, :], centred[:, b, :], ACT.Identity, bias=bias[b], scale=gain[b])
+        halves = [slice(0, CH // 2), slice(CH // 2, CH)]
+        for half in halves:
+            nc.scalar.activation(rstd_row[:, half], sq_row[:, half], ACT.Abs_reciprocal_sqrt, bias=eps[:], scale=1.0)
+        for half in halves:
+            for b in range(KB):
+                if half == halves[0]:
+                    nc.vector.tensor_tensor(centred[:, b, :], centred[:, b, :], mean_row[:], ALU.subtract)
+                nc.vector.tensor_tensor(centred[:, b, half], centred[:, b, half], rstd_row[:, half], ALU.mult)
+                if b == 0:
+                    nc.vector.tensor_scalar(h[0][:, b, half], centred[:, b, half], gain[b], bias[b], ALU.mult, ALU.add)
+                else:
+                    nc.scalar.activation(
+                        h[0][:, b, half], centred[:, b, half], ACT.Identity, bias=bias[b], scale=gain[b]
+                    )
 
         blocks = [(pj, m) for pj in range(3) for m in range(KB)]
         for ch in range(NCH):
@@ -174,15 +179,17 @@ def tile_decoderlm_b_kernel(
 
             for round_blocks in rounds:
                 acc = [psum_acc.tile([P, CH], F32, name=f"acc{pj}_{m}", tag="acc") for pj, m in round_blocks]
-                for kb in range(KB):
-                    for a, (pj, m) in zip(acc, round_blocks):
-                        nc.tensor.matmul(
-                            a[:],
-                            weights[pj][:, kb, m * P : (m + 1) * P],
-                            h[ch][:, kb, :],
-                            start=(kb == 0),
-                            stop=(kb == KB - 1),
-                        )
+                first_round = ch == 0 and round_blocks is rounds[0]
+                for cols in halves if first_round else [slice(0, CH)]:
+                    for kb in range(KB):
+                        for a, (pj, m) in zip(acc, round_blocks):
+                            nc.tensor.matmul(
+                                a[:, cols],
+                                weights[pj][:, kb, m * P : (m + 1) * P],
+                                h[ch][:, kb, cols],
+                                start=(kb == 0),
+                                stop=(kb == KB - 1),
+                            )
                 for a, (pj, m) in zip(acc, round_blocks):
                     col = (2 + pj) * KB + m
                     res = stage.tile([P, CH], F32, name="res")

@@ -17,9 +17,11 @@ N = 1024
 KB = D // P
 CH = 256
 NCH = N // CH
+LEAD = 96
 SQ = 32
-PREP_BANKS = 3
+PREP_BANKS = 2
 ACC_BANKS = 8 - PREP_BANKS
+FIRST_SIDE = ACC_BANKS
 SIDE = 4
 RING = 3
 STAGE = 20
@@ -28,10 +30,10 @@ FLOPS = 3 * 2 * D * D * N
 
 PAIR = 2
 STEP_LOOK_UP = 0
-STEP_MEAN = 10
-STEP_CENTRE = 11
-STEP_VAR = 18
-STEP_SCALE = 19
+STEP_MEAN = 11
+STEP_CENTRE = 12
+STEP_VAR = 20
+STEP_SCALE = 21
 
 
 def tile_decoderlm_b_kernel(
@@ -57,7 +59,11 @@ def tile_decoderlm_b_kernel(
         nc.sync.dma_start(pos[0][:], pos_dram[0])
         for b in range(KB):
             nc.sync.dma_start(tok[b][:], tok_emb[b * P : (b + 1) * P, :])
-        nc.sync.dma_start(weights[0][:], wq.rearrange(by_block, p=P))
+        first_cols = slice(0, FIRST_SIDE * P)
+        for kb in range(0, KB, PAIR):
+            rows = wq[kb * P : (kb + PAIR) * P, first_cols]
+            nc.sync.dma_start(weights[0][:, kb : kb + PAIR, first_cols], rows.rearrange(by_block, p=P))
+        nc.sync.dma_start(weights[0][:, :, FIRST_SIDE * P : D], wq[:, FIRST_SIDE * P : D].rearrange(by_block, p=P))
         nc.sync.dma_start(pos[1][:], pos_dram[1])
         nc.sync.dma_start(weights[1][:], wk.rearrange(by_block, p=P))
         nc.sync.dma_start(weights[2][:], wv.rearrange(by_block, p=P))
@@ -90,7 +96,7 @@ def tile_decoderlm_b_kernel(
             nc.scalar.dma_start(
                 vec_rows[v * KB : (v + 1) * KB, :], vec.rearrange("(kb p) one -> kb (p one)", p=P)
             )
-        vec_flip = psum_prep.tile([P, NV], F32, name="vec_flip", tag="prep")
+        vec_flip = psum_acc.tile([P, NV], F32, name="vec_flip", tag="acc")
         nc.tensor.transpose(vec_flip[:], vec_rows[:], ident[0:NV, 0:NV])
         vec_cols = held.tile([P, NV], F32, name="vec_cols")
         nc.vector.tensor_copy(vec_cols[:], vec_flip[:])
@@ -127,74 +133,114 @@ def tile_decoderlm_b_kernel(
         x[0] = held.tile([P, KB, CH], F32, name="x0", tag="ring0")
         h[0] = held.tile([P, KB, CH], BF16, name="h0", tag="ring1")
 
-        shift_row = psum_prep.tile([P, CH], F32, name="shift_row0", tag="prep")
-        mean_row = psum_prep.tile([P, CH], F32, name="mean_row0", tag="prep")
-        sq_row = psum_prep.tile([P, CH], F32, name="sq_row0", tag="prep")
-        centred = held.tile([P, KB, CH], F32, name="centred0", tag="centred")
+        lead = slice(0, LEAD)
+        rest = slice(LEAD, CH)
+        parts = [lead, rest]
+        widths = [LEAD, CH - LEAD]
+        shift_row = psum_acc.tile([P, CH], F32, name="shift_row0", tag="acc")
+        lead_mean = psum_prep.tile([P, LEAD], F32, name="lead_mean", tag="prep")
+        lead_sq = psum_acc.tile([P, LEAD], F32, name="lead_sq", tag="acc")
+        rest_sums = psum_prep.tile([P, 2, CH - LEAD], F32, name="rest_sums", tag="prep")
+        mean_rows = [lead_mean[:], rest_sums[:, 0, :]]
+        sq_rows = [lead_sq[:], rest_sums[:, 1, :]]
+        both = held.tile([P, KB, 2, CH], F32, name="both")
+        d = [both[:, b, 0, :] for b in range(KB)]
+        sq = [both[:, b, 1, :] for b in range(KB)]
         pos_shifted = held.tile([P, KB, CH], F32, name="pos_shifted")
-        for b in range(KB):
+        rstd_row = x[0][:, KB - 1, :]
+
+        def add_up_lead(b):
+            nc.tensor.matmul(lead_mean[:], averager[:], d[b][:, lead], start=(b == 0), stop=(b == KB - 1))
+            nc.tensor.matmul(lead_sq[:], averager[:], sq[b][:, lead], start=(b == 0), stop=(b == KB - 1))
+
+        def add_up_rest(b):
+            nc.tensor.matmul(rest_sums[:], averager[:], both[:, b, :, rest], start=(b == 0), stop=(b == KB - 1))
+
+        for b in range(KB - 1):
             if b == 0:
                 nc.vector.tensor_tensor(x[0][:, b, :], tok[b][:].indirect(pieces[0]), pos[0][:, b, :], ALU.add)
                 nc.tensor.matmul(shift_row[:], minus_block_averager[:], x[0][:, 0, :], start=True, stop=True)
-                nc.vector.tensor_tensor(centred[:, b, :], x[0][:, b, :], shift_row[:], ALU.add)
+                nc.vector.tensor_tensor(d[b], x[0][:, b, :], shift_row[:], ALU.add)
                 for later in range(1, KB):
                     nc.vector.tensor_tensor(pos_shifted[:, later, :], pos[0][:, later, :], shift_row[:], ALU.add)
             else:
-                nc.vector.tensor_tensor(
-                    centred[:, b, :], tok[b][:].indirect(pieces[0]), pos_shifted[:, b, :], ALU.add
-                )
-            sq = work.tile([P, CH], F32, name="sq")
-            nc.vector.tensor_tensor(sq[:], centred[:, b, :], centred[:, b, :], ALU.mult)
-            nc.tensor.matmul(mean_row[:], averager[:], centred[:, b, :], start=(b == 0), stop=(b == KB - 1))
-            nc.tensor.matmul(sq_row[:], averager[:], sq[:], start=(b == 0), stop=False)
+                nc.vector.tensor_tensor(d[b], tok[b][:].indirect(pieces[0]), pos_shifted[:, b, :], ALU.add)
+            nc.vector.tensor_tensor(sq[b], d[b], d[b], ALU.mult)
+            add_up_lead(b)
+            add_up_rest(b)
             if b > 0:
                 nc.vector.tensor_tensor(x[0][:, b, :], tok[b][:].indirect(pieces[0]), pos[0][:, b, :], ALU.add)
-        nc.sync.dma_start(x_dram[0], x[0][:])
 
-        mean_sq = held.tile([P, CH], F32, name="mean_sq0", tag="mean_sq")
-        nc.scalar.activation(mean_sq[:], mean_row[:], ACT.Square)
-        nc.tensor.matmul(sq_row[:], minus_block_averager[:], mean_sq[:], start=False, stop=True)
-        rstd_row = held.tile([P, CH], F32, name="rstd_row0", tag="rstd_row")
-        halves = [slice(0, CH // 2), slice(CH // 2, CH)]
-        for half in halves:
-            nc.scalar.activation(rstd_row[:, half], sq_row[:, half], ACT.Abs_reciprocal_sqrt, bias=eps[:], scale=1.0)
-        for half in halves:
+        mean_sq = [None, None]
+        for i, part in enumerate(parts):
+            b = KB - 1
+            piece = offsets[:, part.start // 16 : part.stop // 16]
+            nc.vector.tensor_tensor(d[b][:, part], tok[b][:].indirect(piece), pos_shifted[:, b, part], ALU.add)
+            nc.scalar.activation(sq[b][:, part], d[b][:, part], ACT.Square)
+            if i == 0:
+                add_up_lead(b)
+            else:
+                add_up_rest(b)
+            mean_sq[i] = work.tile([P, widths[i]], F32, name=f"mean_sq{i}")
+            nc.scalar.activation(mean_sq[i][:], mean_rows[i], ACT.Square)
+
+        def one_over_std(i):
+            var = work.tile([P, widths[i]], F32, name=f"var{i}")
+            nc.vector.tensor_tensor(var[:], sq_rows[i], mean_sq[i][:], ALU.subtract)
+            nc.scalar.activation(rstd_row[:, parts[i]], var[:], ACT.Abs_reciprocal_sqrt, bias=eps[:], scale=1.0)
+
+        one_over_std(0)
+        for i, part in enumerate(parts):
             for b in range(KB):
-                if half == halves[0]:
-                    nc.vector.tensor_tensor(centred[:, b, :], centred[:, b, :], mean_row[:], ALU.subtract)
-                nc.vector.tensor_tensor(centred[:, b, half], centred[:, b, half], rstd_row[:, half], ALU.mult)
+                if i == 0 and b == PAIR:
+                    one_over_std(1)
+                d_part = d[b][:, part]
+                nc.vector.tensor_tensor(d_part, d_part, mean_rows[i], ALU.subtract)
+                nc.vector.tensor_tensor(d_part, d_part, rstd_row[:, part], ALU.mult)
                 if b == 0:
-                    nc.vector.tensor_scalar(h[0][:, b, half], centred[:, b, half], gain[b], bias[b], ALU.mult, ALU.add)
+                    nc.vector.tensor_scalar(h[0][:, b, part], d_part, gain[b], bias[b], ALU.mult, ALU.add)
                 else:
-                    nc.scalar.activation(
-                        h[0][:, b, half], centred[:, b, half], ACT.Identity, bias=bias[b], scale=gain[b]
-                    )
+                    nc.scalar.activation(h[0][:, b, part], d_part, ACT.Identity, bias=bias[b], scale=gain[b])
+        nc.vector.tensor_tensor(
+            x[0][:, KB - 1, :], tok[KB - 1][:].indirect(pieces[0]), pos[0][:, KB - 1, :], ALU.add
+        )
+        nc.sync.dma_start(x_dram[0], x[0][:])
 
         blocks = [(pj, m) for pj in range(3) for m in range(KB)]
         for ch in range(NCH):
-            rounds = [blocks[0:SIDE]] + [[blk] for blk in blocks[SIDE:]]
+            if ch == 0:
+                rounds = [
+                    (blocks[0:FIRST_SIDE], parts[0], False),
+                    (blocks[0:SIDE], parts[1], True),
+                    (blocks[SIDE:FIRST_SIDE], parts[1], True),
+                ] + [([blk], slice(0, CH), True) for blk in blocks[FIRST_SIDE:]]
+            else:
+                rounds = [(blocks[0:SIDE], slice(0, CH), True)] + [([blk], slice(0, CH), True) for blk in blocks[SIDE:]]
             nx = ch + 1
             x_sum = sq_sum = packed = mean_row = rstd_row = None
             step = 0
+            acc = {}
 
-            for round_blocks in rounds:
-                acc = [psum_acc.tile([P, CH], F32, name=f"acc{pj}_{m}", tag="acc") for pj, m in round_blocks]
-                first_round = ch == 0 and round_blocks is rounds[0]
-                for cols in halves if first_round else [slice(0, CH)]:
-                    for kb in range(KB):
-                        for a, (pj, m) in zip(acc, round_blocks):
-                            nc.tensor.matmul(
-                                a[:, cols],
-                                weights[pj][:, kb, m * P : (m + 1) * P],
-                                h[ch][:, kb, cols],
-                                start=(kb == 0),
-                                stop=(kb == KB - 1),
-                            )
-                for a, (pj, m) in zip(acc, round_blocks):
+            for round_blocks, cols, finished in rounds:
+                for pj, m in round_blocks:
+                    if (pj, m) not in acc:
+                        acc[pj, m] = psum_acc.tile([P, CH], F32, name=f"acc{pj}_{m}", tag="acc")
+                for kb in range(KB):
+                    for pj, m in round_blocks:
+                        nc.tensor.matmul(
+                            acc[pj, m][:, cols],
+                            weights[pj][:, kb, m * P : (m + 1) * P],
+                            h[ch][:, kb, cols],
+                            start=(kb == 0),
+                            stop=(kb == KB - 1),
+                        )
+                if not finished:
+                    continue
+                for pj, m in round_blocks:
                     col = (2 + pj) * KB + m
                     res = stage.tile([P, CH], F32, name="res")
                     nc.scalar.activation(
-                        res[:], a[:], ACT.Identity, bias=vec_cols[:, col : col + 1], scale=1.0
+                        res[:], acc[pj, m][:], ACT.Identity, bias=vec_cols[:, col : col + 1], scale=1.0
                     )
                     row = (1 + pj) * D + m * P
                     nc.sync.dma_start(out[row : row + P, ch * CH : (ch + 1) * CH], res[:])
@@ -232,8 +278,8 @@ def tile_decoderlm_b_kernel(
                     elif step == STEP_VAR:
                         rstd_row = spread(packed, ACT.Abs_reciprocal_sqrt, eps[:], "rstd")
                         h[nx] = held.tile([P, KB, CH], BF16, name=f"h{nx}", tag=f"ring{(2 * nx + 1) % RING}")
-                    elif STEP_SCALE <= step < STEP_SCALE + KB // PAIR:
-                        for b in range((step - STEP_SCALE) * PAIR, (step - STEP_SCALE + 1) * PAIR):
+                    elif STEP_SCALE <= step < STEP_SCALE + 2:
+                        for b in range((step - STEP_SCALE) * KB // 2, (step - STEP_SCALE + 1) * KB // 2):
                             nc.vector.tensor_tensor(centred[:, b, :], centred[:, b, :], rstd_row[:], ALU.mult)
                             nc.scalar.activation(
                                 h[nx][:, b, :], centred[:, b, :], ACT.Identity, bias=bias[b], scale=gain[b]

@@ -59,13 +59,12 @@ def tile_decoderlm_b_kernel(
         nc.sync.dma_start(pos[0][:], pos_dram[0])
         for b in range(KB):
             nc.sync.dma_start(tok[b][:], tok_emb[b * P : (b + 1) * P, :])
-        first_cols = slice(0, FIRST_SIDE * P)
         for kb in range(0, KB, PAIR):
-            rows = wq[kb * P : (kb + PAIR) * P, first_cols]
-            nc.sync.dma_start(weights[0][:, kb : kb + PAIR, first_cols], rows.rearrange(by_block, p=P))
-        nc.sync.dma_start(weights[0][:, :, FIRST_SIDE * P : D], wq[:, FIRST_SIDE * P : D].rearrange(by_block, p=P))
+            rows = wq[kb * P : (kb + PAIR) * P, :]
+            nc.sync.dma_start(weights[0][:, kb : kb + PAIR, :], rows.rearrange(by_block, p=P))
         nc.sync.dma_start(pos[1][:], pos_dram[1])
-        nc.sync.dma_start(weights[1][:], wk.rearrange(by_block, p=P))
+        for outputs in (slice(0, D // 2), slice(D // 2, D)):
+            nc.sync.dma_start(weights[1][:, :, outputs], wk[:, outputs].rearrange(by_block, p=P))
         nc.sync.dma_start(weights[2][:], wv.rearrange(by_block, p=P))
         nc.sync.dma_start(pos[2][:], pos_dram[2])
         nc.sync.dma_start(pos[3][:], pos_dram[3])

from contextlib import ExitStack

import concourse.mybir as mybir
from concourse.masks import make_identity

F32 = mybir.dt.float32
BF16 = mybir.dt.bfloat16
U16 = mybir.dt.uint16
ALU = mybir.AluOpType
ACT = mybir.ActivationFunctionType
AX = mybir.AxisListType

P = 128
D = 1024
V = 2048
N = 1024
KB = D // P
CH = 256
NCH = N // CH
LEAD = 96
SQ = 32
PREP_BANKS = 2
ACC_BANKS = 8 - PREP_BANKS
FIRST_SIDE = ACC_BANKS
SIDE = 4
RING = 3
STAGE = 20
EPS = 1e-5
FLOPS = 3 * 2 * D * D * N

PAIR = 2
STEP_LOOK_UP = 0
STEP_MEAN = 11
STEP_CENTRE = 12
STEP_VAR = 20
STEP_SCALE = 21


def tile_decoderlm_b_kernel(
    tc, tok_emb, pos_enc, ln_gain, ln_bias, wq, bq, wk, bk, wv, bv, offs, out
):
    nc = tc.nc
    with ExitStack() as ctx:
        held = ctx.enter_context(tc.tile_pool(name="held", bufs=1))
        work = ctx.enter_context(tc.tile_pool(name="work", bufs=3))
        stage = ctx.enter_context(tc.tile_pool(name="stage", bufs=STAGE))
        psum_prep = ctx.enter_context(tc.psum_pool(name="psum_prep", bufs=PREP_BANKS))
        psum_acc = ctx.enter_context(tc.psum_pool(name="psum_acc", bufs=ACC_BANKS))

        offsets = held.tile([P, N // 16], U16, name="offsets")
        nc.sync.dma_start(offsets[:], offs)

        tok = [held.tile([P, V], F32, name=f"tok{b}") for b in range(KB)]
        pos = [held.tile([P, KB, CH], F32, name=f"pos{ch}") for ch in range(NCH)]
        weights = [held.tile([P, KB, D], BF16, name=f"w{pj}") for pj in range(3)]
        by_block = "(kb p) n -> p kb n"
        pos_dram = [pos_enc[:, ch * CH : (ch + 1) * CH].rearrange(by_block, p=P) for ch in range(NCH)]

        nc.sync.dma_start(pos[0][:], pos_dram[0])
        for b in range(KB):
            nc.sync.dma_start(tok[b][:], tok_emb[b * P : (b + 1) * P, :])
        for kb in range(0, KB, PAIR):
            rows = wq[kb * P : (kb + PAIR) * P, :]
            nc.sync.dma_start(weights[0][:, kb : kb + PAIR, :], rows.rearrange(by_block, p=P))
        nc.sync.dma_start(pos[1][:], pos_dram[1])
        for outputs in (slice(0, D // 2), slice(D // 2, D)):
            nc.sync.dma_start(weights[1][:, :, outputs], wk[:, outputs].rearrange(by_block, p=P))
        nc.sync.dma_start(weights[2][:], wv.rearrange(by_block, p=P))
        nc.sync.dma_start(pos[2][:], pos_dram[2])
        nc.sync.dma_start(pos[3][:], pos_dram[3])

        ident = held.tile([P, P], F32, name="ident")
        make_identity(nc, ident[:])
        averager = held.tile([P, P], F32, name="averager")
        nc.vector.memset(averager[:], 1.0 / D)
        minus_block_averager = held.tile([P, P], F32, name="minus_block_averager")
        nc.vector.memset(minus_block_averager[:], -1.0 / P)
        strip = held.tile([P, SQ], F32, name="strip")
        nc.vector.tensor_reduce(strip[:], ident[:].rearrange("p (c j) -> p j c", j=SQ), AX.X, ALU.add)
        fold = held.tile([P, P], F32, name="fold")
        nc.vector.tensor_scalar_mul(
            fold[:].rearrange("p (c j) -> p c j", j=SQ),
            strip[:].unsqueeze(1).to_broadcast([P, P // SQ, SQ]),
            1.0 / D,
        )
        eps = held.tile([P, 1], F32, name="eps")
        nc.vector.memset(eps[:], EPS)
        table_warm = held.tile([P, 1], F32, name="table_warm")
        nc.scalar.activation(table_warm[:], eps[:], ACT.Abs_reciprocal_sqrt)

        vectors = (ln_gain, ln_bias, bq, bk, bv)
        NV = len(vectors) * KB
        vec_rows = held.tile([NV, P], F32, name="vec_rows")
        for v, vec in enumerate(vectors):
            nc.scalar.dma_start(
                vec_rows[v * KB : (v + 1) * KB, :], vec.rearrange("(kb p) one -> kb (p one)", p=P)
            )
        vec_flip = psum_acc.tile([P, NV], F32, name="vec_flip", tag="acc")
        nc.tensor.transpose(vec_flip[:], vec_rows[:], ident[0:NV, 0:NV])
        vec_cols = held.tile([P, NV], F32, name="vec_cols")
        nc.vector.tensor_copy(vec_cols[:], vec_flip[:])
        gain = [vec_cols[:, b : b + 1] for b in range(KB)]
        bias = [vec_cols[:, KB + b : KB + b + 1] for b in range(KB)]

        def pack(total, what):
            flipped = held.tile([P, CH], F32, name=f"flipped_{what}", tag="flipped", align_bytes=64)
            nc.vector.transpose(flipped[:], total[:])
            packed = held.tile([P, CH // SQ], F32, name=f"packed_{what}", tag="packed")
            nc.vector.tensor_reduce(packed[:], flipped[:].rearrange("p (c j) -> p c j", j=SQ), AX.X, ALU.add)
            return packed

        def spread(packed, func, func_bias, what):
            means = psum_prep.tile([P, CH // SQ], F32, name=f"means_{what}", tag="prep")
            nc.tensor.matmul(means[:], fold[:], packed[:], start=True, stop=True)
            repeated = held.tile([P, CH], F32, name=f"repeated_{what}", tag="repeated", align_bytes=64)
            nc.scalar.activation(
                repeated[:].rearrange("p (c j) -> p c j", j=SQ),
                means[:].unsqueeze(2).to_broadcast([P, CH // SQ, SQ]),
                func,
                bias=func_bias,
                scale=1.0,
            )
            row = held.tile([P, CH], F32, name=f"row_{what}", tag=f"row_{what}", align_bytes=64)
            nc.vector.transpose(row[:], repeated[:])
            return row

        pieces = [offsets[:, ch * (CH // 16) : (ch + 1) * (CH // 16)] for ch in range(NCH)]
        x_dram = [out[0:D, ch * CH : (ch + 1) * CH].rearrange(by_block, p=P) for ch in range(NCH)]

        x = [None] * NCH
        h = [None] * NCH
        x[0] = held.tile([P, KB, CH], F32, name="x0", tag="ring0")
        h[0] = held.tile([P, KB, CH], BF16, name="h0", tag="ring1")

        lead = slice(0, LEAD)
        rest = slice(LEAD, CH)
        parts = [lead, rest]
        widths = [LEAD, CH - LEAD]
        shift_row = psum_acc.tile([P, CH], F32, name="shift_row0", tag="acc")
        lead_mean = psum_prep.tile([P, LEAD], F32, name="lead_mean", tag="prep")
        lead_sq = psum_acc.tile([P, LEAD], F32, name="lead_sq", tag="acc")
        rest_sums = psum_prep.tile([P, 2, CH - LEAD], F32, name="rest_sums", tag="prep")
        mean_rows = [lead_mean[:], rest_sums[:, 0, :]]
        sq_rows = [lead_sq[:], rest_sums[:, 1, :]]
        both = held.tile([P, KB, 2, CH], F32, name="both")
        d = [both[:, b, 0, :] for b in range(KB)]
        sq = [both[:, b, 1, :] for b in range(KB)]
        pos_shifted = held.tile([P, KB, CH], F32, name="pos_shifted")
        rstd_row = x[0][:, KB - 1, :]

        def add_up_lead(b):
            nc.tensor.matmul(lead_mean[:], averager[:], d[b][:, lead], start=(b == 0), stop=(b == KB - 1))
            nc.tensor.matmul(lead_sq[:], averager[:], sq[b][:, lead], start=(b == 0), stop=(b == KB - 1))

        def add_up_rest(b):
            nc.tensor.matmul(rest_sums[:], averager[:], both[:, b, :, rest], start=(b == 0), stop=(b == KB - 1))

        for b in range(KB - 1):
            if b == 0:
                nc.vector.tensor_tensor(x[0][:, b, :], tok[b][:].indirect(pieces[0]), pos[0][:, b, :], ALU.add)
                nc.tensor.matmul(shift_row[:], minus_block_averager[:], x[0][:, 0, :], start=True, stop=True)
                nc.vector.tensor_tensor(d[b], x[0][:, b, :], shift_row[:], ALU.add)
                for later in range(1, KB):
                    nc.vector.tensor_tensor(pos_shifted[:, later, :], pos[0][:, later, :], shift_row[:], ALU.add)
            else:
                nc.vector.tensor_tensor(d[b], tok[b][:].indirect(pieces[0]), pos_shifted[:, b, :], ALU.add)
            nc.vector.tensor_tensor(sq[b], d[b], d[b], ALU.mult)
            add_up_lead(b)
            add_up_rest(b)
            if b > 0:
                nc.vector.tensor_tensor(x[0][:, b, :], tok[b][:].indirect(pieces[0]), pos[0][:, b, :], ALU.add)

        mean_sq = [None, None]
        for i, part in enumerate(parts):
            b = KB - 1
            piece = offsets[:, part.start // 16 : part.stop // 16]
            nc.vector.tensor_tensor(d[b][:, part], tok[b][:].indirect(piece), pos_shifted[:, b, part], ALU.add)
            nc.scalar.activation(sq[b][:, part], d[b][:, part], ACT.Square)
            if i == 0:
                add_up_lead(b)
            else:
                add_up_rest(b)
            mean_sq[i] = work.tile([P, widths[i]], F32, name=f"mean_sq{i}")
            nc.scalar.activation(mean_sq[i][:], mean_rows[i], ACT.Square)

        def one_over_std(i):
            var = work.tile([P, widths[i]], F32, name=f"var{i}")
            nc.vector.tensor_tensor(var[:], sq_rows[i], mean_sq[i][:], ALU.subtract)
            nc.scalar.activation(rstd_row[:, parts[i]], var[:], ACT.Abs_reciprocal_sqrt, bias=eps[:], scale=1.0)

        one_over_std(0)
        for i, part in enumerate(parts):
            for b in range(KB):
                if i == 0 and b == PAIR:
                    one_over_std(1)
                d_part = d[b][:, part]
                nc.vector.tensor_tensor(d_part, d_part, mean_rows[i], ALU.subtract)
                nc.vector.tensor_tensor(d_part, d_part, rstd_row[:, part], ALU.mult)
                if b == 0:
                    nc.vector.tensor_scalar(h[0][:, b, part], d_part, gain[b], bias[b], ALU.mult, ALU.add)
                else:
                    nc.scalar.activation(h[0][:, b, part], d_part, ACT.Identity, bias=bias[b], scale=gain[b])
        nc.vector.tensor_tensor(
            x[0][:, KB - 1, :], tok[KB - 1][:].indirect(pieces[0]), pos[0][:, KB - 1, :], ALU.add
        )
        nc.sync.dma_start(x_dram[0], x[0][:])

        blocks = [(pj, m) for pj in range(3) for m in range(KB)]
        for ch in range(NCH):
            if ch == 0:
                rounds = [
                    (blocks[0:FIRST_SIDE], parts[0], False),
                    (blocks[0:SIDE], parts[1], True),
                    (blocks[SIDE:FIRST_SIDE], parts[1], True),
                ] + [([blk], slice(0, CH), True) for blk in blocks[FIRST_SIDE:]]
            else:
                rounds = [(blocks[0:SIDE], slice(0, CH), True)] + [([blk], slice(0, CH), True) for blk in blocks[SIDE:]]
            nx = ch + 1
            x_sum = sq_sum = packed = mean_row = rstd_row = None
            step = 0
            acc = {}

            for round_blocks, cols, finished in rounds:
                for pj, m in round_blocks:
                    if (pj, m) not in acc:
                        acc[pj, m] = psum_acc.tile([P, CH], F32, name=f"acc{pj}_{m}", tag="acc")
                for kb in range(KB):
                    for pj, m in round_blocks:
                        nc.tensor.matmul(
                            acc[pj, m][:, cols],
                            weights[pj][:, kb, m * P : (m + 1) * P],
                            h[ch][:, kb, cols],
                            start=(kb == 0),
                            stop=(kb == KB - 1),
                        )
                if not finished:
                    continue
                for pj, m in round_blocks:
                    col = (2 + pj) * KB + m
                    res = stage.tile([P, CH], F32, name="res")
                    nc.scalar.activation(
                        res[:], acc[pj, m][:], ACT.Identity, bias=vec_cols[:, col : col + 1], scale=1.0
                    )
                    row = (1 + pj) * D + m * P
                    nc.sync.dma_start(out[row : row + P, ch * CH : (ch + 1) * CH], res[:])

                for blk in round_blocks:
                    if nx == NCH:
                        break
                    if step == STEP_LOOK_UP:
                        x[nx] = held.tile([P, KB, CH], F32, name=f"x{nx}", tag=f"ring{(2 * nx) % RING}")
                        x_sum = held.tile([P, CH], F32, name=f"x_sum{nx}", tag="x_sum", align_bytes=64)
                        for b in range(KB):
                            nc.vector.tensor_tensor(
                                x[nx][:, b, :], tok[b][:].indirect(pieces[nx]), pos[nx][:, b, :], ALU.add
                            )
                            if b > 0:
                                so_far = x[nx][:, 0, :] if b == 1 else x_sum[:]
                                nc.vector.tensor_tensor(x_sum[:], so_far, x[nx][:, b, :], ALU.add)
                        nc.sync.dma_start(x_dram[nx], x[nx][:])
                        packed = pack(x_sum, "mean")
                    elif step == STEP_MEAN:
                        mean_row = spread(packed, ACT.Identity, 0.0, "mean")
                        centred = held.tile([P, KB, CH], F32, name=f"centred{nx}", tag="centred")
                        sq_sum = held.tile([P, CH], F32, name=f"sq_sum{nx}", tag="sq_sum", align_bytes=64)
                    elif STEP_CENTRE <= step < STEP_CENTRE + KB // PAIR:
                        for b in range((step - STEP_CENTRE) * PAIR, (step - STEP_CENTRE + 1) * PAIR):
                            nc.vector.tensor_tensor(centred[:, b, :], x[nx][:, b, :], mean_row[:], ALU.subtract)
                            if b == 0:
                                nc.scalar.activation(sq_sum[:], centred[:, b, :], ACT.Square)
                            else:
                                sq = work.tile([P, CH], F32, name="sq")
                                nc.scalar.activation(sq[:], centred[:, b, :], ACT.Square)
                                nc.vector.tensor_tensor(sq_sum[:], sq_sum[:], sq[:], ALU.add)
                        if step == STEP_CENTRE + KB // PAIR - 1:
                            packed = pack(sq_sum, "var")
                    elif step == STEP_VAR:
                        rstd_row = spread(packed, ACT.Abs_reciprocal_sqrt, eps[:], "rstd")
                        h[nx] = held.tile([P, KB, CH], BF16, name=f"h{nx}", tag=f"ring{(2 * nx + 1) % RING}")
                    elif STEP_SCALE <= step < STEP_SCALE + 2:
                        for b in range((step - STEP_SCALE) * KB // 2, (step - STEP_SCALE + 1) * KB // 2):
                            nc.vector.tensor_tensor(centred[:, b, :], centred[:, b, :], rstd_row[:], ALU.mult)
                            nc.scalar.activation(
                                h[nx][:, b, :], centred[:, b, :], ACT.Identity, bias=bias[b], scale=gain[b]
                            )
                    step += 1
